import numpy as np
import ml_dtypes


def mxq(x, axis, fmt="e4m3"):
    dtype, down = {"e4m3": (ml_dtypes.float8_e4m3fn, 7), "e5m2": (ml_dtypes.float8_e5m2, 14)}[fmt]
    v = np.moveaxis(np.asarray(x, np.float32).astype(ml_dtypes.bfloat16).astype(np.float64), axis, -1)
    blocks = v.reshape(v.shape[:-1] + (-1, 32))
    amax = np.abs(blocks).max(-1, keepdims=True)
    byte = np.maximum(np.where(amax > 0, np.frexp(amax)[1] - 1 + 127, 0) - down, 1)
    scale = np.exp2(byte - 127.0)
    codes = (blocks / scale).astype(np.float32).astype(dtype).astype(np.float64)
    return np.moveaxis((codes * scale).reshape(v.shape), -1, axis)


WIDE = False


def mx_kscale(k):
    if not WIDE:
        return np.ones(k)
    levels = np.array([10, -10, 5, -5, 0])
    a = np.random.permutation(np.resize(levels, k // 512 * 4)).reshape(k // 512, 4)
    idx = np.arange(k)
    return np.exp2(a[idx // 512, idx % 128 // 32])


BF16 = ml_dtypes.bfloat16


def bf(x):
    return np.asarray(x, np.float32).astype(BF16)


def f64(x):
    return np.asarray(x).astype(np.float64)


WAY, SHOT, QUERY_SHOT, D, M = 4, 6, 8, 640, 512
G, Q = 4, 5
NS, NQ = WAY * SHOT, WAY * QUERY_SHOT


def log_softmax(v, axis):
    z = v - v.max(axis, keepdims=True)
    return z - np.log(np.exp(z).sum(axis, keepdims=True))


def setup_inputs():
    s = mx_kscale(M)
    return {"feature_map": bf(np.random.standard_normal((NS + NQ, D, M)) * np.sqrt(M) * s),
            "weight2": bf(np.random.uniform(0.0, 1.0, (NS, NQ, M)) / s),
            "scale": bf(G * Q * Q * SHOT / np.sqrt(D) * (1.0 + 0.1 * np.random.standard_normal(1)))}


def reference(feature_map, weight2, scale):
    fq = mxq(f64(feature_map), 2, "e4m3")
    wq = mxq(f64(weight2), 2, "e4m3")
    support = fq[:NS]
    query = fq[NS:]
    centroid = (wq @ support.transpose(0, 2, 1)) / M
    query_r = (wq.transpose(1, 0, 2) @ query.transpose(0, 2, 1)).transpose(1, 0, 2) / M
    l2 = ((centroid - query_r) ** 2).sum(-1)
    neg_l2 = -l2.T
    logits = neg_l2 / (G * Q * Q * SHOT) * f64(scale)
    return log_softmax(logits, 1)

@@ -1,0 +1,312 @@
+from contextlib import ExitStack
+
+import concourse.mybir as mybir
+from concourse.masks import make_identity
+
+FLOPS = 2 * 2 * 24 * 32 * 640 * 512
+
+F32 = mybir.dt.float32
+BF16 = mybir.dt.bfloat16
+U32 = mybir.dt.uint32
+U8 = mybir.dt.uint8
+I32 = mybir.dt.int32
+FP8X4 = mybir.dt.float8_e4m3fn_x4
+ALU = mybir.AluOpType
+ACT = mybir.ActivationFunctionType
+AX = mybir.AxisListType
+
+P = 128
+NS = 24
+NQ = 32
+DC = 5
+X_BUFS = 16
+L2_FIRST = 15
+LOGIT_FACTOR = -1.0 / (600.0 * 512.0 * 512.0)
+
+
+def pair_list(count):
+    pairs = []
+    for t in range(count // 4):
+        pairs.append((4 * t, 4 * t + 2))
+        pairs.append((4 * t + 1, 4 * t + 3))
+    return pairs
+
+
+def tile_proto_kernel(tc, feature_map, weight2, scale, out):
+    nc = tc.nc
+    cycles = [(False, a, b) for a, b in pair_list(NS)] + [(True, a, b) for a, b in pair_list(NQ)]
+    n_cyc = len(cycles)
+
+    with ExitStack() as ctx:
+        const = ctx.enter_context(tc.tile_pool(name="const", bufs=1))
+        xin = ctx.enter_context(tc.tile_pool(name="xin", bufs=X_BUFS))
+        gpool = ctx.enter_context(tc.tile_pool(name="gpool", bufs=3))
+        qpool = ctx.enter_context(tc.tile_pool(name="qpool", bufs=3))
+        psum = ctx.enter_context(tc.psum_pool(name="psum", bufs=1))
+        ctx.enter_context(tc.manual_schedule())
+
+        x_tiles = {}
+        t_banks = {}
+        grouped = {}
+        quant = {}
+        m_banks = {}
+
+        def load(k):
+            is_q, a, b = cycles[k]
+            tiles = []
+            for idx in (a, b):
+                img = idx + (NS if is_q else 0)
+                xt = xin.tile([P, DC * 512], BF16)
+                nc.sync.dma_start(out=xt[:], in_=feature_map[img].rearrange("(p c) m -> p (c m)", c=DC))
+                tiles.append(xt)
+            x_tiles[k] = tiles
+
+        def copy_words(on_scalar, dst, src):
+            if on_scalar:
+                nc.scalar.copy(out=dst, in_=src)
+            else:
+                nc.vector.tensor_copy(out=dst, in_=src)
+
+        w_in = const.tile([P, 6, 512], BF16)
+        nc.sync.dma_start(
+            out=w_in[:],
+            in_=weight2.rearrange("s q m -> (s q) m").rearrange("(j p) m -> p j m", p=P),
+        )
+        sc_bf = const.tile([P, 1], BF16)
+        nc.scalar.dma_start(out=sc_bf[:], in_=scale.partition_broadcast(P))
+        for k in range(X_BUFS // 2):
+            load(k)
+
+        ident = const.tile([P, P], F32)
+        make_identity(nc, ident[:])
+        diff = const.tile([P, DC * 1024], F32)
+        nc.gpsimd.memset(diff[:], 0.0)
+
+        warm = const.tile([P, 1], F32)
+        nc.vector.memset(warm[:], 0.0)
+        nc.scalar.activation(out=warm[:], in_=warm[:], func=ACT.Exp)
+
+        wg1 = const.tile([P, 768 * 4], BF16, align_bytes=64)
+        wg2 = const.tile([P, 1024 * 4], BF16, align_bytes=64)
+        w1c = const.tile([P, 832], U32, align_bytes=64)
+        w1s = const.tile([P, 832], U8, align_bytes=64)
+        w2c = const.tile([P, 1088], U32, align_bytes=64)
+        w2s = const.tile([P, 1088], U8, align_bytes=64)
+        c_sb = const.tile([P, DC * NS * NQ], F32)
+        l2_sb = const.tile([P, P], F32)
+        ones = const.tile([P, 2], F32)
+        sc_f = const.tile([P, 1], F32)
+
+        nc.vector.memset(wg2[:].bitcast(F32), 0.0)
+        nc.vector.memset(w1c[:, 768:832].bitcast(I32), 0)
+        nc.vector.memset(w1s[:, 768:832].bitcast(I32), 0)
+        nc.vector.memset(w2c[:, 1024:1088].bitcast(I32), 0)
+        nc.vector.memset(w2s[:, 1024:1088].bitcast(I32), 0)
+        nc.vector.memset(l2_sb[:], 0.0)
+        nc.vector.memset(ones[:], 1.0)
+        nc.vector.tensor_scalar(out=sc_f[:], in0=sc_bf[:], scalar1=LOGIT_FACTOR, scalar2=None, op0=ALU.mult)
+
+        cv = c_sb[:].rearrange("p (c s q) -> p c s q", c=DC, s=NS, q=NQ)
+        dv = diff[:].rearrange("p (c n s i) -> p c n s i", c=DC, n=16, s=32, i=2)
+
+        w32 = w_in[:].bitcast(F32)
+        wg1_32 = wg1[:].bitcast(F32)
+        wg2_v = wg2[:].bitcast(F32).rearrange("p (q s u) -> p q s u", q=32, s=32, u=2)
+        for b in range(3):
+            wb = psum.tile([P, 512], F32, tag="m%d" % b)
+            for cl in range(2):
+                for u in range(2):
+                    nc.tensor.transpose(
+                        wb[:, (2 * cl + u) * P : (2 * cl + u + 1) * P],
+                        w32[:, 2 * b + cl, u * P : (u + 1) * P],
+                        ident[:],
+                    )
+            on_scalar = b != 1
+            copy_words(
+                on_scalar,
+                wg1_32[:, b * 512 : (b + 1) * 512].rearrange("p (c d u) -> p c d u", c=2, d=P, u=2),
+                wb[:].rearrange("p (c u d) -> p c d u", c=2, u=2, d=P),
+            )
+            wb_v = wb[:].rearrange("p (c u s q) -> p c q s u", c=2, u=2, s=4, q=32)
+            for cl in range(2):
+                j = 2 * b + cl
+                copy_words(on_scalar, wg2_v[:, :, 4 * j : 4 * j + 4, :], wb_v[:, cl])
+        nc.vector.quantize_mx(out=w1c[:, 0:512].bitcast(FP8X4), scales=w1s[:, 0:512], in_=wg1[:, 0:2048])
+        nc.vector.quantize_mx(out=w1c[:, 512:768].bitcast(FP8X4), scales=w1s[:, 512:768], in_=wg1[:, 2048:3072])
+        nc.vector.quantize_mx(out=w2c[:, 0:1024].bitcast(FP8X4), scales=w2s[:, 0:1024], in_=wg2[:, 0:4096])
+
+        def transposes(k):
+            banks = []
+            for b in range(5):
+                tb = psum.tile([P, 512], F32, tag="t%d" % b)
+                for cl in range(2):
+                    g = 2 * b + cl
+                    x32 = x_tiles[k][g // DC][:].bitcast(F32)
+                    dc = g % DC
+                    for u in range(2):
+                        nc.tensor.transpose(
+                            tb[:, (2 * cl + u) * P : (2 * cl + u + 1) * P],
+                            x32[:, dc * 256 + u * P : dc * 256 + (u + 1) * P],
+                            ident[:],
+                        )
+                banks.append(tb)
+            t_banks[k] = banks
+
+        def copy_bank(k, b, on_scalar):
+            g32 = grouped[k][:].bitcast(F32)
+            copy_words(
+                on_scalar,
+                g32[:, b * 512 : (b + 1) * 512].rearrange("p (c d u) -> p c d u", c=2, d=P, u=2),
+                t_banks[k][b][:].rearrange("p (c u d) -> p c d u", c=2, u=2, d=P),
+            )
+
+        def copies_scalar(k):
+            gr = gpool.tile([P, 10 * 512], BF16, align_bytes=64)
+            grouped[k] = gr
+            for b in range(4):
+                copy_bank(k, b, True)
+
+        def copies_vector(k):
+            copy_bank(k, 4, False)
+
+        def quantise(k):
+            codes = qpool.tile([P, 1280], U32, align_bytes=64)
+            planes = qpool.tile([P, 1280], U8, align_bytes=64)
+            gr = grouped[k]
+            nc.vector.quantize_mx(out=codes[:, 0:1024].bitcast(FP8X4), scales=planes[:, 0:1024], in_=gr[:, 0:4096])
+            nc.vector.quantize_mx(
+                out=codes[:, 1024:1280].bitcast(FP8X4), scales=planes[:, 1024:1280], in_=gr[:, 4096:5120]
+            )
+            quant[k] = (codes, planes)
+
+        def l2_matmuls(t, bank):
+            for dc in range(DC):
+                nc.tensor.matmul(
+                    out=bank[:, 256:258],
+                    lhsT=diff[:, dc * 1024 + t * P : dc * 1024 + (t + 1) * P],
+                    rhs=ones[:],
+                    start=(dc == 0),
+                    stop=(dc == DC - 1),
+                )
+
+        def l2_copy(t, bank):
+            nc.vector.tensor_copy(out=l2_sb[:, t : t + 1], in_=bank[:, 256:257])
+
+        def mx_passes(k, l2_chunk):
+            is_q, a, b = cycles[k]
+            codes, planes = quant[k]
+            wc, ws = (w2c, w2s) if is_q else (w1c, w1s)
+            banks = []
+            for mbi in range(3):
+                mb = psum.tile([P, 512], F32, tag="m%d" % mbi)
+                banks.append(mb)
+            for dc in range(DC):
+                for i, idx in enumerate((a, b)):
+                    g = i * DC + dc
+                    w0 = 64 * (idx // 2)
+                    pos = (dc % 2) * 2 + i
+                    nc.tensor.matmul_mx(
+                        out=banks[dc // 2][:, pos * P : (pos + 1) * P],
+                        lhsT=codes[:, g * P : (g + 1) * P].bitcast(FP8X4),
+                        lhsT_scale=planes[:, g * P : (g + 1) * P],
+                        rhs=wc[:, w0 : w0 + P].bitcast(FP8X4),
+                        rhs_scale=ws[:, w0 : w0 + P],
+                        start=True,
+                        stop=True,
+                    )
+            if l2_chunk is not None:
+                l2_matmuls(l2_chunk, banks[2])
+            m_banks[k] = (banks, l2_chunk)
+
+        def drain(k):
+            is_q, a, b = cycles[k]
+            banks, l2_chunk = m_banks[k]
+            off = 32 * (a % 2)
+            n = (a // 4) * 2 + a % 4
+            for mbi in range(3):
+                if mbi < 2:
+                    c0 = 2 * mbi
+                    if is_q:
+                        nc.vector.tensor_tensor(
+                            out=dv[:, c0 : c0 + 2, n, 0:NS, :],
+                            in0=cv[:, c0 : c0 + 2, :, a : b + 1 : 2],
+                            in1=banks[mbi][:].rearrange("p (c i r) -> p c r i", c=2, i=2, r=P)[:, :, off : off + NS, :],
+                            op=ALU.subtract,
+                        )
+                    else:
+                        nc.vector.tensor_copy(
+                            out=cv[:, c0 : c0 + 2, a : b + 1 : 2, :],
+                            in_=banks[mbi][:].rearrange("p (c i r) -> p c i r", c=2, i=2, r=P)[:, :, :, off : off + NQ],
+                        )
+                else:
+                    if is_q:
+                        nc.vector.tensor_tensor(
+                            out=dv[:, 4, n, 0:NS, :],
+                            in0=cv[:, 4, :, a : b + 1 : 2],
+                            in1=banks[2][:, 0:256].rearrange("p (i r) -> p r i", i=2, r=P)[:, off : off + NS, :],
+                            op=ALU.subtract,
+                        )
+                    else:
+                        nc.vector.tensor_copy(
+                            out=cv[:, 4, a : b + 1 : 2, :],
+                            in_=banks[2][:, 0:256].rearrange("p (i r) -> p i r", i=2, r=P)[:, :, off : off + NQ],
+                        )
+            if l2_chunk is not None:
+                l2_copy(l2_chunk, banks[2])
+
+        def square(k):
+            is_q, a, b = cycles[k]
+            n = (a // 4) * 2 + a % 4
+            nc.scalar.activation(out=dv[:, :, n, 0:NS, :], in_=dv[:, :, n, 0:NS, :], func=ACT.Square)
+
+        for k in range(n_cyc + 3):
+            if 0 <= k - 3 < n_cyc:
+                drain(k - 3)
+            if k < n_cyc:
+                transposes(k)
+                if k + X_BUFS // 2 < n_cyc:
+                    load(k + X_BUFS // 2)
+                copies_scalar(k)
+            if 0 <= k - 1 < n_cyc:
+                quantise(k - 1)
+            if k < n_cyc:
+                copies_vector(k)
+            if 0 <= k - 2 < n_cyc:
+                kx = k - 2
+                chunk = None
+                if kx >= L2_FIRST and (kx - L2_FIRST) % 2 == 0:
+                    chunk = (kx - L2_FIRST) // 2
+                mx_passes(kx, chunk)
+            if 0 <= k - 3 < n_cyc and cycles[k - 3][0]:
+                square(k - 3)
+
+        last = psum.tile([P, 512], F32, tag="m2")
+        l2_matmuls(7, last)
+        l2_copy(7, last)
+
+        fin = psum.tile([P, 512], F32, tag="t0")
+        nc.tensor.transpose(fin[:, 0:P], l2_sb[:], ident[:])
+        z = const.tile([P, 4, NS], F32)
+        zs = const.tile([P, 4, NS], F32)
+        ez = const.tile([P, 4, NS], F32)
+        res = const.tile([P, 4, NS], F32)
+        mx = const.tile([P, 4], F32)
+        sm = const.tile([P, 4], F32)
+        ls = const.tile([P, 4], F32)
+        nc.vector.tensor_scalar(
+            out=z[:].rearrange("p (i n) s -> p i n s", i=2, n=2),
+            in0=fin[:, 0:P].rearrange("p (n s i) -> p i n s", n=2, s=32, i=2)[:, :, :, 0:NS],
+            scalar1=sc_f[:, 0:1],
+            scalar2=None,
+            op0=ALU.mult,
+        )
+        nc.vector.tensor_reduce(out=mx[:], in_=z[:], axis=AX.X, op=ALU.max)
+        nc.vector.tensor_tensor(out=zs[:], in0=z[:], in1=mx[:].unsqueeze(2).to_broadcast([P, 4, NS]), op=ALU.subtract)
+        nc.scalar.activation(out=ez[:], in_=zs[:], func=ACT.Exp)
+        nc.vector.tensor_reduce(out=sm[:], in_=ez[:], axis=AX.X, op=ALU.add)
+        nc.scalar.activation(out=ls[:], in_=sm[:], func=ACT.Ln)
+        nc.vector.tensor_tensor(out=res[:], in0=zs[:], in1=ls[:].unsqueeze(2).to_broadcast([P, 4, NS]), op=ALU.subtract)
+        nc.sync.dma_start(
+            out=out.rearrange("(t l) s -> t (l s)", l=4),
+            in_=res[0:8].rearrange("p l s -> p (l s)"),
+        )

@@ -20,46 +20,56 @@ NS = 24
 NQ = 32
 DC = 5
 X_BUFS = 16
-L2_FIRST = 15
+SLOT = 64
+LAG = 2
+BLK = 32
 LOGIT_FACTOR = -1.0 / (600.0 * 512.0 * 512.0)
 
-
-def pair_list(count):
-    pairs = []
-    for t in range(count // 4):
-        pairs.append((4 * t, 4 * t + 2))
-        pairs.append((4 * t + 1, 4 * t + 3))
-    return pairs
+PIECES = {2: (8, 2), 1: (4, 1)}
+VECTOR_BANKS = {2: (4,), 1: (1,)}
+SUPPORT_QUAD = ((2, 2),)
+QUERY_QUADS = (((2, 2),),) * 7 + (((2,), (1,), (1,)),)
 
 
 def tile_proto_kernel(tc, feature_map, weight2, scale, out):
     nc = tc.nc
-    cycles = [(False, a, b) for a, b in pair_list(NS)] + [(True, a, b) for a, b in pair_list(NQ)]
-    n_cyc = len(cycles)
+    loads = []
+    passes = []
+    images = []
+    for is_q, quads in ((False, (SUPPORT_QUAD,) * (NS // 4)), (True, QUERY_QUADS)):
+        for t, quad in enumerate(quads):
+            h0 = 0
+            for group in quad:
+                members = []
+                for n in group:
+                    members.append(len(loads))
+                    loads.append((len(images), n))
+                    for il in range(n):
+                        images.append(4 * t + h0 + sum(loads[m][1] for m in members[:-1]) + il + (NS if is_q else 0))
+                total = sum(group)
+                passes.append((is_q, t, h0, total, members))
+                h0 += total
+    n_loads = len(loads)
+    pass_after = {}
+    for x, entry in enumerate(passes):
+        pass_after[entry[4][-1]] = x
 
     with ExitStack() as ctx:
         const = ctx.enter_context(tc.tile_pool(name="const", bufs=1))
         xin = ctx.enter_context(tc.tile_pool(name="xin", bufs=X_BUFS))
-        gpool = ctx.enter_context(tc.tile_pool(name="gpool", bufs=3))
-        qpool = ctx.enter_context(tc.tile_pool(name="qpool", bufs=3))
-        psum = ctx.enter_context(tc.psum_pool(name="psum", bufs=1))
+        gpool = ctx.enter_context(tc.tile_pool(name="gpool", bufs=6))
+        qpool = ctx.enter_context(tc.tile_pool(name="qpool", bufs=8))
+        tpool = ctx.enter_context(tc.psum_pool(name="tpool", bufs=5))
+        mpool = ctx.enter_context(tc.psum_pool(name="mpool", bufs=1))
         ctx.enter_context(tc.manual_schedule())
 
-        x_tiles = {}
-        t_banks = {}
-        grouped = {}
-        quant = {}
-        m_banks = {}
+        x_tiles = []
 
-        def load(k):
-            is_q, a, b = cycles[k]
-            tiles = []
-            for idx in (a, b):
-                img = idx + (NS if is_q else 0)
-                xt = xin.tile([P, DC * 512], BF16)
-                nc.sync.dma_start(out=xt[:], in_=feature_map[img].rearrange("(p c) m -> p (c m)", c=DC))
-                tiles.append(xt)
-            x_tiles[k] = tiles
+        def load_next():
+            img = images[len(x_tiles)]
+            xt = xin.tile([P, DC * 512], BF16)
+            nc.sync.dma_start(out=xt[:], in_=feature_map[img].rearrange("(p c) m -> p (c m)", c=DC))
+            x_tiles.append(xt)
 
         def copy_words(on_scalar, dst, src):
             if on_scalar:
@@ -74,46 +84,51 @@ def tile_proto_kernel(tc, feature_map, weight2, scale, out):
         )
         sc_bf = const.tile([P, 1], BF16)
         nc.scalar.dma_start(out=sc_bf[:], in_=scale.partition_broadcast(P))
-        for k in range(X_BUFS // 2):
-            load(k)
+        for k in range(X_BUFS):
+            load_next()
 
         ident = const.tile([P, P], F32)
         make_identity(nc, ident[:])
-        diff = const.tile([P, DC * 1024], F32)
-        nc.gpsimd.memset(diff[:], 0.0)
+        diffs = []
+        for r in range(3):
+            dt_r = const.tile([P, DC * P], F32, name="diff%d" % r)
+            nc.gpsimd.memset(dt_r[:], 0.0)
+            diffs.append(dt_r)
 
         warm = const.tile([P, 1], F32)
         nc.vector.memset(warm[:], 0.0)
         nc.scalar.activation(out=warm[:], in_=warm[:], func=ACT.Exp)
 
-        wg1 = const.tile([P, 768 * 4], BF16, align_bytes=64)
-        wg2 = const.tile([P, 1024 * 4], BF16, align_bytes=64)
-        w1c = const.tile([P, 832], U32, align_bytes=64)
-        w1s = const.tile([P, 832], U8, align_bytes=64)
-        w2c = const.tile([P, 1088], U32, align_bytes=64)
-        w2s = const.tile([P, 1088], U8, align_bytes=64)
-        c_sb = const.tile([P, DC * NS * NQ], F32)
+        w1c = const.tile([P, (NS + 1) * SLOT], U32, align_bytes=64)
+        w1s = const.tile([P, (NS + 1) * SLOT], U8, align_bytes=64)
+        w2c = const.tile([P, (NQ + 1) * SLOT], U32, align_bytes=64)
+        w2s = const.tile([P, (NQ + 1) * SLOT], U8, align_bytes=64)
+        c_sb = const.tile([P, DC * NQ * NS], F32)
         l2_sb = const.tile([P, P], F32)
         ones = const.tile([P, 2], F32)
         sc_f = const.tile([P, 1], F32)
+        cv = c_sb[:].rearrange("p (c q s) -> p c q s", c=DC, q=NQ, s=NS)
 
-        nc.vector.memset(wg2[:].bitcast(F32), 0.0)
-        nc.vector.memset(w1c[:, 768:832].bitcast(I32), 0)
-        nc.vector.memset(w1s[:, 768:832].bitcast(I32), 0)
-        nc.vector.memset(w2c[:, 1024:1088].bitcast(I32), 0)
-        nc.vector.memset(w2s[:, 1024:1088].bitcast(I32), 0)
+        wg = []
+        for r in range(4):
+            wg_r = gpool.tile([P, 4096], BF16, align_bytes=64, tag="grouped", name="wg%d" % r)
+            wg.append(wg_r)
+        wgv = [w[:].bitcast(F32).rearrange("p (l c u) -> p l c u", l=16, c=SLOT, u=2) for w in wg]
+        nc.vector.memset(wgv[0][:, :, NQ:SLOT, :], 0.0)
+        nc.vector.memset(wgv[1][:, 0:8, NQ:SLOT, :], 0.0)
+        nc.vector.memset(wgv[2][:, :, NS:SLOT, :], 0.0)
+        nc.vector.memset(wgv[3][:, :, NS:SLOT, :], 0.0)
+        nc.vector.memset(w1c[:, NS * SLOT :].bitcast(I32), 0)
+        nc.vector.memset(w1s[:, NS * SLOT :].bitcast(I32), 0)
+        nc.vector.memset(w2c[:, NQ * SLOT :].bitcast(I32), 0)
+        nc.vector.memset(w2s[:, NQ * SLOT :].bitcast(I32), 0)
         nc.vector.memset(l2_sb[:], 0.0)
         nc.vector.memset(ones[:], 1.0)
         nc.vector.tensor_scalar(out=sc_f[:], in0=sc_bf[:], scalar1=LOGIT_FACTOR, scalar2=None, op0=ALU.mult)
 
-        cv = c_sb[:].rearrange("p (c s q) -> p c s q", c=DC, s=NS, q=NQ)
-        dv = diff[:].rearrange("p (c n s i) -> p c n s i", c=DC, n=16, s=32, i=2)
-
         w32 = w_in[:].bitcast(F32)
-        wg1_32 = wg1[:].bitcast(F32)
-        wg2_v = wg2[:].bitcast(F32).rearrange("p (q s u) -> p q s u", q=32, s=32, u=2)
         for b in range(3):
-            wb = psum.tile([P, 512], F32, tag="m%d" % b)
+            wb = tpool.tile([P, 512], F32, tag="tb")
             for cl in range(2):
                 for u in range(2):
                     nc.tensor.transpose(
@@ -122,68 +137,88 @@ def tile_proto_kernel(tc, feature_map, weight2, scale, out):
                         ident[:],
                     )
             on_scalar = b != 1
-            copy_words(
-                on_scalar,
-                wg1_32[:, b * 512 : (b + 1) * 512].rearrange("p (c d u) -> p c d u", c=2, d=P, u=2),
-                wb[:].rearrange("p (c u d) -> p c d u", c=2, u=2, d=P),
-            )
-            wb_v = wb[:].rearrange("p (c u s q) -> p c q s u", c=2, u=2, s=4, q=32)
+            wb_sq = wb[:].rearrange("p (c u s q) -> p c s q u", c=2, u=2, s=4, q=NQ)
+            wb_qs = wb[:].rearrange("p (c u s q) -> p c q s u", c=2, u=2, s=4, q=NQ)
             for cl in range(2):
                 j = 2 * b + cl
-                copy_words(on_scalar, wg2_v[:, :, 4 * j : 4 * j + 4, :], wb_v[:, cl])
-        nc.vector.quantize_mx(out=w1c[:, 0:512].bitcast(FP8X4), scales=w1s[:, 0:512], in_=wg1[:, 0:2048])
-        nc.vector.quantize_mx(out=w1c[:, 512:768].bitcast(FP8X4), scales=w1s[:, 512:768], in_=wg1[:, 2048:3072])
-        nc.vector.quantize_mx(out=w2c[:, 0:1024].bitcast(FP8X4), scales=w2s[:, 0:1024], in_=wg2[:, 0:4096])
+                s0 = 4 * j
+                copy_words(on_scalar, wgv[s0 // 16][:, s0 % 16 : s0 % 16 + 4, 0:NQ, :], wb_sq[:, cl])
+                for half in range(2):
+                    copy_words(
+                        on_scalar,
+                        wgv[2 + half][:, :, s0 : s0 + 4, :],
+                        wb_qs[:, cl, 16 * half : 16 * half + 16],
+                    )
+        nc.vector.quantize_mx(out=w1c[:, 0:1024].bitcast(FP8X4), scales=w1s[:, 0:1024], in_=wg[0][:])
+        nc.vector.quantize_mx(out=w1c[:, 1024:1536].bitcast(FP8X4), scales=w1s[:, 1024:1536], in_=wg[1][:, 0:2048])
+        nc.vector.quantize_mx(out=w2c[:, 0:1024].bitcast(FP8X4), scales=w2s[:, 0:1024], in_=wg[2][:])
+        nc.vector.quantize_mx(out=w2c[:, 1024:2048].bitcast(FP8X4), scales=w2s[:, 1024:2048], in_=wg[3][:])
+
+        t_banks = {}
+        grouped = {}
+        quant = {}
+        m_banks = {}
+
+        def piece_of(n, g):
+            start = 0
+            for pi, size in enumerate(PIECES[n]):
+                if g < start + size:
+                    return pi, g - start
+                start += size
+            return None
 
         def transposes(k):
+            first, n = loads[k]
             banks = []
-            for b in range(5):
-                tb = psum.tile([P, 512], F32, tag="t%d" % b)
-                for cl in range(2):
+            for b in range((DC * n + 1) // 2):
+                tb = tpool.tile([P, 512], F32, tag="tb")
+                for cl in range(min(2, DC * n - 2 * b)):
                     g = 2 * b + cl
-                    x32 = x_tiles[k][g // DC][:].bitcast(F32)
+                    x32 = x_tiles[first + g // DC][:].bitcast(F32)
                     dc = g % DC
-                    for u in range(2):
+                    for h in range(2):
                         nc.tensor.transpose(
-                            tb[:, (2 * cl + u) * P : (2 * cl + u + 1) * P],
-                            x32[:, dc * 256 + u * P : dc * 256 + (u + 1) * P],
+                            tb[:, (2 * cl + h) * P : (2 * cl + h + 1) * P],
+                            x32[:, dc * 256 + h * P : dc * 256 + (h + 1) * P],
                             ident[:],
                         )
                 banks.append(tb)
             t_banks[k] = banks
+            tiles = []
+            for pi in range(len(PIECES[n])):
+                gr = gpool.tile([P, 4096], BF16, align_bytes=64, tag="grouped")
+                tiles.append(gr)
+            grouped[k] = tiles
 
-        def copy_bank(k, b, on_scalar):
-            g32 = grouped[k][:].bitcast(F32)
+        def copy_bank(k, b):
+            n = loads[k][1]
+            chunks = min(2, DC * n - 2 * b)
+            pi, c0 = piece_of(n, 2 * b)
+            g32 = grouped[k][pi][:].bitcast(F32)
             copy_words(
-                on_scalar,
-                g32[:, b * 512 : (b + 1) * 512].rearrange("p (c d u) -> p c d u", c=2, d=P, u=2),
-                t_banks[k][b][:].rearrange("p (c u d) -> p c d u", c=2, u=2, d=P),
+                b not in VECTOR_BANKS[n],
+                g32[:, c0 * 256 : (c0 + chunks) * 256].rearrange("p (c d h) -> p c d h", c=chunks, d=P, h=2),
+                t_banks[k][b][:, 0 : chunks * 256].rearrange("p (c h d) -> p c d h", c=chunks, h=2, d=P),
             )
 
-        def copies_scalar(k):
-            gr = gpool.tile([P, 10 * 512], BF16, align_bytes=64)
-            grouped[k] = gr
-            for b in range(4):
-                copy_bank(k, b, True)
-
-        def copies_vector(k):
-            copy_bank(k, 4, False)
-
-        def quantise(k):
-            codes = qpool.tile([P, 1280], U32, align_bytes=64)
-            planes = qpool.tile([P, 1280], U8, align_bytes=64)
-            gr = grouped[k]
-            nc.vector.quantize_mx(out=codes[:, 0:1024].bitcast(FP8X4), scales=planes[:, 0:1024], in_=gr[:, 0:4096])
+        def quantise(k, pi):
+            size = PIECES[loads[k][1]][pi]
+            codes = qpool.tile([P, 1024], U32, align_bytes=64)
+            planes = qpool.tile([P, 1024], U8, align_bytes=64)
             nc.vector.quantize_mx(
-                out=codes[:, 1024:1280].bitcast(FP8X4), scales=planes[:, 1024:1280], in_=gr[:, 4096:5120]
+                out=codes[:, 0 : size * P].bitcast(FP8X4),
+                scales=planes[:, 0 : size * P],
+                in_=grouped[k][pi][:, 0 : size * 512],
             )
-            quant[k] = (codes, planes)
+            if pi == 0:
+                quant[k] = []
+            quant[k].append((codes, planes))
 
         def l2_matmuls(t, bank):
             for dc in range(DC):
                 nc.tensor.matmul(
                     out=bank[:, 256:258],
-                    lhsT=diff[:, dc * 1024 + t * P : dc * 1024 + (t + 1) * P],
+                    lhsT=diffs[t % 3][:, dc * P : (dc + 1) * P],
                     rhs=ones[:],
                     start=(dc == 0),
                     stop=(dc == DC - 1),
@@ -192,99 +227,113 @@ def tile_proto_kernel(tc, feature_map, weight2, scale, out):
         def l2_copy(t, bank):
             nc.vector.tensor_copy(out=l2_sb[:, t : t + 1], in_=bank[:, 256:257])
 
-        def mx_passes(k, l2_chunk):
-            is_q, a, b = cycles[k]
-            codes, planes = quant[k]
+        def mx_passes(x):
+            is_q, t, h0, n, members = passes[x]
             wc, ws = (w2c, w2s) if is_q else (w1c, w1s)
+            where = []
+            for k in members:
+                for il in range(loads[k][1]):
+                    where.append((k, il))
             banks = []
             for mbi in range(3):
-                mb = psum.tile([P, 512], F32, tag="m%d" % mbi)
+                mb = mpool.tile([P, 512], F32, tag="m%d" % mbi)
                 banks.append(mb)
             for dc in range(DC):
-                for i, idx in enumerate((a, b)):
-                    g = i * DC + dc
-                    w0 = 64 * (idx // 2)
-                    pos = (dc % 2) * 2 + i
+                for i in range(n):
+                    k, il = where[i]
+                    pi, c0 = piece_of(loads[k][1], il * DC + dc)
+                    codes, planes = quant[k][pi]
+                    w0 = SLOT * (4 * t + h0 + i)
+                    col = BLK * ((dc % 2) * n + i)
                     nc.tensor.matmul_mx(
-                        out=banks[dc // 2][:, pos * P : (pos + 1) * P],
-                        lhsT=codes[:, g * P : (g + 1) * P].bitcast(FP8X4),
-                        lhsT_scale=planes[:, g * P : (g + 1) * P],
+                        out=banks[dc // 2][:, col : col + P],
+                        lhsT=codes[:, c0 * P : (c0 + 1) * P].bitcast(FP8X4),
+                        lhsT_scale=planes[:, c0 * P : (c0 + 1) * P],
                         rhs=wc[:, w0 : w0 + P].bitcast(FP8X4),
                         rhs_scale=ws[:, w0 : w0 + P],
                         start=True,
                         stop=True,
                     )
-            if l2_chunk is not None:
-                l2_matmuls(l2_chunk, banks[2])
-            m_banks[k] = (banks, l2_chunk)
+            m_banks[x] = banks
 
-        def drain(k):
-            is_q, a, b = cycles[k]
-            banks, l2_chunk = m_banks[k]
-            off = 32 * (a % 2)
-            n = (a // 4) * 2 + a % 4
-            for mbi in range(3):
-                if mbi < 2:
-                    c0 = 2 * mbi
-                    if is_q:
-                        nc.vector.tensor_tensor(
-                            out=dv[:, c0 : c0 + 2, n, 0:NS, :],
-                            in0=cv[:, c0 : c0 + 2, :, a : b + 1 : 2],
-                            in1=banks[mbi][:].rearrange("p (c i r) -> p c r i", c=2, i=2, r=P)[:, :, off : off + NS, :],
-                            op=ALU.subtract,
-                        )
-                    else:
-                        nc.vector.tensor_copy(
-                            out=cv[:, c0 : c0 + 2, a : b + 1 : 2, :],
-                            in_=banks[mbi][:].rearrange("p (c i r) -> p c i r", c=2, i=2, r=P)[:, :, :, off : off + NQ],
-                        )
+        def drain(x):
+            is_q, t, h0, n, members = passes[x]
+            banks = m_banks[x]
+            q0 = 4 * t + h0
+            dv = diffs[t % 3][:].rearrange("p (c i s) -> p c i s", c=DC, i=4, s=32)
+            for mbi in range(2):
+                c0 = 2 * mbi
+                if is_q:
+                    nc.vector.tensor_tensor(
+                        out=dv[:, c0 : c0 + 2, h0 : h0 + n, 0:NS],
+                        in0=cv[:, c0 : c0 + 2, q0 : q0 + n, :],
+                        in1=banks[mbi][:, 0 : 2 * n * BLK].rearrange("p (c i r) -> p c i r", c=2, i=n, r=BLK)[:, :, :, 0:NS],
+                        op=ALU.subtract,
+                    )
                 else:
-                    if is_q:
-                        nc.vector.tensor_tensor(
-                            out=dv[:, 4, n, 0:NS, :],
-                            in0=cv[:, 4, :, a : b + 1 : 2],
-                            in1=banks[2][:, 0:256].rearrange("p (i r) -> p r i", i=2, r=P)[:, off : off + NS, :],
-                            op=ALU.subtract,
-                        )
-                    else:
-                        nc.vector.tensor_copy(
-                            out=cv[:, 4, a : b + 1 : 2, :],
-                            in_=banks[2][:, 0:256].rearrange("p (i r) -> p i r", i=2, r=P)[:, :, off : off + NQ],
-                        )
-            if l2_chunk is not None:
-                l2_copy(l2_chunk, banks[2])
+                    nc.vector.tensor_copy(
+                        out=cv[:, c0 : c0 + 2, :, q0 : q0 + n],
+                        in_=banks[mbi][:, 0 : 2 * n * BLK].rearrange("p (c i r) -> p c r i", c=2, i=n, r=BLK),
+                    )
+            if is_q:
+                nc.vector.tensor_tensor(
+                    out=dv[:, 4, h0 : h0 + n, 0:NS],
+                    in0=cv[:, 4, q0 : q0 + n, :],
+                    in1=banks[2][:, 0 : n * BLK].rearrange("p (i r) -> p i r", i=n, r=BLK)[:, :, 0:NS],
+                    op=ALU.subtract,
+                )
+            else:
+                nc.vector.tensor_copy(
+                    out=cv[:, 4, :, q0 : q0 + n],
+                    in_=banks[2][:, 0 : n * BLK].rearrange("p (i r) -> p r i", i=n, r=BLK),
+                )
 
-        def square(k):
-            is_q, a, b = cycles[k]
-            n = (a // 4) * 2 + a % 4
-            nc.scalar.activation(out=dv[:, :, n, 0:NS, :], in_=dv[:, :, n, 0:NS, :], func=ACT.Square)
+        def square(x):
+            is_q, t, h0, n, members = passes[x]
+            dv = diffs[t % 3][:].rearrange("p (c i s) -> p c i s", c=DC, i=4, s=32)
+            nc.scalar.activation(out=dv[:, :, h0 : h0 + n, 0:NS], in_=dv[:, :, h0 : h0 + n, 0:NS], func=ACT.Square)
 
-        for k in range(n_cyc + 3):
-            if 0 <= k - 3 < n_cyc:
-                drain(k - 3)
-            if k < n_cyc:
+        to_drain = []
+        to_copy = []
+        to_sum = []
+        latest = None
+        for k in range(n_loads + LAG + 3):
+            drained = to_drain
+            to_drain = []
+            for x in drained:
+                drain(x)
+            for t, bank in to_copy:
+                l2_copy(t, bank)
+            to_copy = []
+            if k < n_loads:
+                n = loads[k][1]
                 transposes(k)
-                if k + X_BUFS // 2 < n_cyc:
-                    load(k + X_BUFS // 2)
-                copies_scalar(k)
-            if 0 <= k - 1 < n_cyc:
-                quantise(k - 1)
-            if k < n_cyc:
-                copies_vector(k)
-            if 0 <= k - 2 < n_cyc:
-                kx = k - 2
-                chunk = None
-                if kx >= L2_FIRST and (kx - L2_FIRST) % 2 == 0:
-                    chunk = (kx - L2_FIRST) // 2
-                mx_passes(kx, chunk)
-            if 0 <= k - 3 < n_cyc and cycles[k - 3][0]:
-                square(k - 3)
+                for il in range(n):
+                    if len(x_tiles) < len(images):
+                        load_next()
+            if 0 <= k - 1 < n_loads:
+                quantise(k - 1, 0)
+                quantise(k - 1, 1)
+            if k < n_loads:
+                for b in range((DC * n + 1) // 2):
+                    copy_bank(k, b)
+            for x in drained:
+                if passes[x][0]:
+                    square(x)
+            if k - LAG in pass_after:
+                latest = pass_after[k - LAG]
+                mx_passes(latest)
+                to_drain.append(latest)
+            for t in to_sum:
+                l2_matmuls(t, m_banks[latest][2])
+                to_copy.append((t, m_banks[latest][2]))
+            to_sum = []
+            for x in drained:
+                is_q, t, h0, n, members = passes[x]
+                if is_q and h0 + n == 4:
+                    to_sum.append(t)
 
-        last = psum.tile([P, 512], F32, tag="m2")
-        l2_matmuls(7, last)
-        l2_copy(7, last)
-
-        fin = psum.tile([P, 512], F32, tag="t0")
+        fin = mpool.tile([P, 512], F32, tag="m0")
         nc.tensor.transpose(fin[:, 0:P], l2_sb[:], ident[:])
         z = const.tile([P, 4, NS], F32)
         zs = const.tile([P, 4, NS], F32)
@@ -294,8 +343,8 @@ def tile_proto_kernel(tc, feature_map, weight2, scale, out):
         sm = const.tile([P, 4], F32)
         ls = const.tile([P, 4], F32)
         nc.vector.tensor_scalar(
-            out=z[:].rearrange("p (i n) s -> p i n s", i=2, n=2),
-            in0=fin[:, 0:P].rearrange("p (n s i) -> p i n s", n=2, s=32, i=2)[:, :, :, 0:NS],
+            out=z[:],
+            in0=fin[:, 0:P].rearrange("p (i s) -> p i s", i=4, s=32)[:, :, 0:NS],
             scalar1=sc_f[:, 0:1],
             scalar2=None,
             op0=ALU.mult,

@@ -19,16 +19,17 @@ P = 128
 NS = 24
 NQ = 32
 DC = 5
-X_BUFS = 16
+X_BUFS = 14
 SLOT = 64
 LAG = 2
 BLK = 32
 LOGIT_FACTOR = -1.0 / (600.0 * 512.0 * 512.0)
 
 PIECES = {2: (8, 2), 1: (4, 1)}
-VECTOR_BANKS = {2: (4,), 1: (1,)}
-SUPPORT_QUAD = ((2, 2),)
-QUERY_QUADS = (((2, 2),),) * 7 + (((2,), (1,), (1,)),)
+VECTOR_BANKS = {2: (4,), 1: (2,)}
+FULL_QUAD = ((2, 2),)
+QUERY_QUADS = (FULL_QUAD,) * 7 + (((2,), (1, 1)),)
+W2_SLOTS = (2, 3)
 
 
 def tile_proto_kernel(tc, feature_map, weight2, scale, out):
@@ -36,7 +37,7 @@ def tile_proto_kernel(tc, feature_map, weight2, scale, out):
     loads = []
     passes = []
     images = []
-    for is_q, quads in ((False, (SUPPORT_QUAD,) * (NS // 4)), (True, QUERY_QUADS)):
+    for is_q, quads in ((False, (FULL_QUAD,) * (NS // 4)), (True, QUERY_QUADS)):
         for t, quad in enumerate(quads):
             h0 = 0
             for group in quad:
@@ -50,17 +51,23 @@ def tile_proto_kernel(tc, feature_map, weight2, scale, out):
                 passes.append((is_q, t, h0, total, members))
                 h0 += total
     n_loads = len(loads)
-    pass_after = {}
+    runs = []
     for x, entry in enumerate(passes):
-        pass_after[entry[4][-1]] = x
+        ready = entry[4][-1] + LAG
+        if entry[3] == 4:
+            runs.append((x, 0, 2, 3, ready))
+            runs.append((x, 1, 2, 2, ready))
+        else:
+            runs.append((x, 0, 1, DC, ready))
 
     with ExitStack() as ctx:
         const = ctx.enter_context(tc.tile_pool(name="const", bufs=1))
         xin = ctx.enter_context(tc.tile_pool(name="xin", bufs=X_BUFS))
-        gpool = ctx.enter_context(tc.tile_pool(name="gpool", bufs=6))
-        qpool = ctx.enter_context(tc.tile_pool(name="qpool", bufs=8))
-        tpool = ctx.enter_context(tc.psum_pool(name="tpool", bufs=5))
+        gpool = ctx.enter_context(tc.tile_pool(name="gpool", bufs=4))
+        qpool = ctx.enter_context(tc.tile_pool(name="qpool", bufs=5))
+        tpool = ctx.enter_context(tc.psum_pool(name="tpool", bufs=6))
         mpool = ctx.enter_context(tc.psum_pool(name="mpool", bufs=1))
+        jpool = ctx.enter_context(tc.tile_pool(name="jpool", bufs=2))
         ctx.enter_context(tc.manual_schedule())
 
         x_tiles = []
@@ -105,25 +112,24 @@ def tile_proto_kernel(tc, feature_map, weight2, scale, out):
         w2s = const.tile([P, (NQ + 1) * SLOT], U8, align_bytes=64)
         c_sb = const.tile([P, DC * NQ * NS], F32)
         l2_sb = const.tile([P, P], F32)
-        ones = const.tile([P, 2], F32)
+        acc = const.tile([P, 2, 8], F32)
         sc_f = const.tile([P, 1], F32)
         cv = c_sb[:].rearrange("p (c q s) -> p c q s", c=DC, q=NQ, s=NS)
 
         wg = []
-        for r in range(4):
-            wg_r = gpool.tile([P, 4096], BF16, align_bytes=64, tag="grouped", name="wg%d" % r)
+        for r, slots in enumerate((16, 8, 16, 16)):
+            wg_r = const.tile([P, slots * SLOT * 4], BF16, align_bytes=64, name="wg%d" % r)
             wg.append(wg_r)
-        wgv = [w[:].bitcast(F32).rearrange("p (l c u) -> p l c u", l=16, c=SLOT, u=2) for w in wg]
+        wgv = [w[:].bitcast(F32).rearrange("p (l c u) -> p l c u", c=SLOT, u=2) for w in wg]
         nc.vector.memset(wgv[0][:, :, NQ:SLOT, :], 0.0)
-        nc.vector.memset(wgv[1][:, 0:8, NQ:SLOT, :], 0.0)
-        nc.vector.memset(wgv[2][:, :, NS:SLOT, :], 0.0)
-        nc.vector.memset(wgv[3][:, :, NS:SLOT, :], 0.0)
+        nc.vector.memset(wgv[1][:, :, NQ:SLOT, :], 0.0)
         nc.vector.memset(w1c[:, NS * SLOT :].bitcast(I32), 0)
         nc.vector.memset(w1s[:, NS * SLOT :].bitcast(I32), 0)
+        nc.vector.memset(wgv[2][:, :, NS:SLOT, :], 0.0)
+        nc.vector.memset(wgv[3][:, :, NS:SLOT, :], 0.0)
         nc.vector.memset(w2c[:, NQ * SLOT :].bitcast(I32), 0)
         nc.vector.memset(w2s[:, NQ * SLOT :].bitcast(I32), 0)
         nc.vector.memset(l2_sb[:], 0.0)
-        nc.vector.memset(ones[:], 1.0)
         nc.vector.tensor_scalar(out=sc_f[:], in0=sc_bf[:], scalar1=LOGIT_FACTOR, scalar2=None, op0=ALU.mult)
 
         w32 = w_in[:].bitcast(F32)
@@ -150,14 +156,13 @@ def tile_proto_kernel(tc, feature_map, weight2, scale, out):
                         wb_qs[:, cl, 16 * half : 16 * half + 16],
                     )
         nc.vector.quantize_mx(out=w1c[:, 0:1024].bitcast(FP8X4), scales=w1s[:, 0:1024], in_=wg[0][:])
-        nc.vector.quantize_mx(out=w1c[:, 1024:1536].bitcast(FP8X4), scales=w1s[:, 1024:1536], in_=wg[1][:, 0:2048])
-        nc.vector.quantize_mx(out=w2c[:, 0:1024].bitcast(FP8X4), scales=w2s[:, 0:1024], in_=wg[2][:])
-        nc.vector.quantize_mx(out=w2c[:, 1024:2048].bitcast(FP8X4), scales=w2s[:, 1024:2048], in_=wg[3][:])
+        nc.vector.quantize_mx(out=w1c[:, 1024:1536].bitcast(FP8X4), scales=w1s[:, 1024:1536], in_=wg[1][:])
 
         t_banks = {}
         grouped = {}
         quant = {}
-        m_banks = {}
+        m_bank = {}
+        turned = {}
 
         def piece_of(n, g):
             start = 0
@@ -184,11 +189,9 @@ def tile_proto_kernel(tc, feature_map, weight2, scale, out):
                         )
                 banks.append(tb)
             t_banks[k] = banks
-            tiles = []
-            for pi in range(len(PIECES[n])):
-                gr = gpool.tile([P, 4096], BF16, align_bytes=64, tag="grouped")
-                tiles.append(gr)
-            grouped[k] = tiles
+            g_big = gpool.tile([P, 4096], BF16, align_bytes=64)
+            g_small = gpool.tile([P, 1024], BF16, align_bytes=64)
+            grouped[k] = (g_big, g_small)
 
         def copy_bank(k, b):
             n = loads[k][1]
@@ -201,52 +204,59 @@ def tile_proto_kernel(tc, feature_map, weight2, scale, out):
                 t_banks[k][b][:, 0 : chunks * 256].rearrange("p (c h d) -> p c d h", c=chunks, h=2, d=P),
             )
 
-        def quantise(k, pi):
-            size = PIECES[loads[k][1]][pi]
-            codes = qpool.tile([P, 1024], U32, align_bytes=64)
-            planes = qpool.tile([P, 1024], U8, align_bytes=64)
-            nc.vector.quantize_mx(
-                out=codes[:, 0 : size * P].bitcast(FP8X4),
-                scales=planes[:, 0 : size * P],
-                in_=grouped[k][pi][:, 0 : size * 512],
-            )
-            if pi == 0:
-                quant[k] = []
-            quant[k].append((codes, planes))
-
-        def l2_matmuls(t, bank):
-            for dc in range(DC):
-                nc.tensor.matmul(
-                    out=bank[:, 256:258],
-                    lhsT=diffs[t % 3][:, dc * P : (dc + 1) * P],
-                    rhs=ones[:],
-                    start=(dc == 0),
-                    stop=(dc == DC - 1),
+        def quantise(k):
+            sizes = PIECES[loads[k][1]]
+            c_big = qpool.tile([P, 1024], U32, align_bytes=64)
+            p_big = qpool.tile([P, 1024], U8, align_bytes=64)
+            c_small = qpool.tile([P, 256], U32, align_bytes=64)
+            p_small = qpool.tile([P, 256], U8, align_bytes=64)
+            quant[k] = ((c_big, p_big), (c_small, p_small))
+            for pi, size in enumerate(sizes):
+                codes, planes = quant[k][pi]
+                nc.vector.quantize_mx(
+                    out=codes[:, 0 : size * P].bitcast(FP8X4),
+                    scales=planes[:, 0 : size * P],
+                    in_=grouped[k][pi][:, 0 : size * 512],
                 )
 
-        def l2_copy(t, bank):
-            nc.vector.tensor_copy(out=l2_sb[:, t : t + 1], in_=bank[:, 256:257])
+        def sum_squares(t):
+            for part, (c0, c1) in enumerate(((0, 4), (4, DC))):
+                dt_ps = tpool.tile([P, 512], F32, tag="tb")
+                for dc in range(c0, c1):
+                    nc.tensor.transpose(
+                        dt_ps[:, (dc - c0) * P : (dc - c0 + 1) * P], diffs[t % 3][:, dc * P : (dc + 1) * P], ident[:]
+                    )
+                turned[(t, part)] = dt_ps
 
-        def mx_passes(x):
+        def square_sums(t):
+            for part, width in enumerate((4 * P, P)):
+                junk = jpool.tile([P, 512], F32)
+                nc.scalar.activation(
+                    out=junk[:, 0:width],
+                    in_=turned[(t, part)][:, 0:width],
+                    func=ACT.Square,
+                    accum_out=acc[:, part, t : t + 1],
+                )
+
+        def mx_run(j):
+            x, d0, step, count, ready = runs[j]
             is_q, t, h0, n, members = passes[x]
             wc, ws = (w2c, w2s) if is_q else (w1c, w1s)
             where = []
             for k in members:
                 for il in range(loads[k][1]):
                     where.append((k, il))
-            banks = []
-            for mbi in range(3):
-                mb = mpool.tile([P, 512], F32, tag="m%d" % mbi)
-                banks.append(mb)
-            for dc in range(DC):
+            mb = mpool.tile([P, 512], F32, tag="m%d" % (j % 2))
+            for row in range(count):
+                dc = d0 + step * row
                 for i in range(n):
                     k, il = where[i]
                     pi, c0 = piece_of(loads[k][1], il * DC + dc)
                     codes, planes = quant[k][pi]
                     w0 = SLOT * (4 * t + h0 + i)
-                    col = BLK * ((dc % 2) * n + i)
+                    col = BLK * (row * n + i)
                     nc.tensor.matmul_mx(
-                        out=banks[dc // 2][:, col : col + P],
+                        out=mb[:, col : col + P],
                         lhsT=codes[:, c0 * P : (c0 + 1) * P].bitcast(FP8X4),
                         lhsT_scale=planes[:, c0 * P : (c0 + 1) * P],
                         rhs=wc[:, w0 : w0 + P].bitcast(FP8X4),
@@ -254,85 +264,85 @@ def tile_proto_kernel(tc, feature_map, weight2, scale, out):
                         start=True,
                         stop=True,
                     )
-            m_banks[x] = banks
+            m_bank[j] = mb
 
-        def drain(x):
+        def diff_view(j):
+            x, d0, step, count, ready = runs[j]
             is_q, t, h0, n, members = passes[x]
-            banks = m_banks[x]
-            q0 = 4 * t + h0
             dv = diffs[t % 3][:].rearrange("p (c i s) -> p c i s", c=DC, i=4, s=32)
-            for mbi in range(2):
-                c0 = 2 * mbi
-                if is_q:
-                    nc.vector.tensor_tensor(
-                        out=dv[:, c0 : c0 + 2, h0 : h0 + n, 0:NS],
-                        in0=cv[:, c0 : c0 + 2, q0 : q0 + n, :],
-                        in1=banks[mbi][:, 0 : 2 * n * BLK].rearrange("p (c i r) -> p c i r", c=2, i=n, r=BLK)[:, :, :, 0:NS],
-                        op=ALU.subtract,
-                    )
-                else:
-                    nc.vector.tensor_copy(
-                        out=cv[:, c0 : c0 + 2, :, q0 : q0 + n],
-                        in_=banks[mbi][:, 0 : 2 * n * BLK].rearrange("p (c i r) -> p c r i", c=2, i=n, r=BLK),
-                    )
+            return dv[:, d0 : d0 + step * (count - 1) + 1 : step, h0 : h0 + n, 0:NS]
+
+        def drain(j):
+            x, d0, step, count, ready = runs[j]
+            is_q, t, h0, n, members = passes[x]
+            first = 4 * t + h0
+            stop = d0 + step * (count - 1) + 1
+            used = m_bank[j][:, 0 : count * n * BLK]
             if is_q:
                 nc.vector.tensor_tensor(
-                    out=dv[:, 4, h0 : h0 + n, 0:NS],
-                    in0=cv[:, 4, q0 : q0 + n, :],
-                    in1=banks[2][:, 0 : n * BLK].rearrange("p (i r) -> p i r", i=n, r=BLK)[:, :, 0:NS],
+                    out=diff_view(j),
+                    in0=cv[:, d0:stop:step, first : first + n, :],
+                    in1=used.rearrange("p (c i r) -> p c i r", c=count, i=n, r=BLK)[:, :, :, 0:NS],
                     op=ALU.subtract,
                 )
             else:
                 nc.vector.tensor_copy(
-                    out=cv[:, 4, :, q0 : q0 + n],
-                    in_=banks[2][:, 0 : n * BLK].rearrange("p (i r) -> p r i", i=n, r=BLK),
+                    out=cv[:, d0:stop:step, :, first : first + n],
+                    in_=used.rearrange("p (c i r) -> p c r i", c=count, i=n, r=BLK),
                 )
 
-        def square(x):
-            is_q, t, h0, n, members = passes[x]
-            dv = diffs[t % 3][:].rearrange("p (c i s) -> p c i s", c=DC, i=4, s=32)
-            nc.scalar.activation(out=dv[:, :, h0 : h0 + n, 0:NS], in_=dv[:, :, h0 : h0 + n, 0:NS], func=ACT.Square)
-
         to_drain = []
-        to_copy = []
-        to_sum = []
-        latest = None
-        for k in range(n_loads + LAG + 3):
+        next_run = 0
+        waiting = []
+        for k in range(n_loads + 8):
+            ending = k >= n_loads - 1
+            if ending and 0 <= k - 1 < n_loads:
+                quantise(k - 1)
             drained = to_drain
             to_drain = []
-            for x in drained:
-                drain(x)
-            for t, bank in to_copy:
-                l2_copy(t, bank)
-            to_copy = []
+            for j in drained:
+                drain(j)
+            complete = []
+            for j in drained:
+                x = runs[j][0]
+                is_q, t, h0, n4, members = passes[x]
+                if is_q and h0 + n4 == 4 and (j + 1 == len(runs) or runs[j + 1][0] != x):
+                    complete.append(t)
             if k < n_loads:
                 n = loads[k][1]
                 transposes(k)
                 for il in range(n):
                     if len(x_tiles) < len(images):
                         load_next()
-            if 0 <= k - 1 < n_loads:
-                quantise(k - 1, 0)
-                quantise(k - 1, 1)
+            if not ending and 0 <= k - 1:
+                quantise(k - 1)
+            if k in W2_SLOTS:
+                half = W2_SLOTS.index(k)
+                nc.vector.quantize_mx(
+                    out=w2c[:, 1024 * half : 1024 * half + 1024].bitcast(FP8X4),
+                    scales=w2s[:, 1024 * half : 1024 * half + 1024],
+                    in_=wg[2 + half][:],
+                )
             if k < n_loads:
                 for b in range((DC * n + 1) // 2):
                     copy_bank(k, b)
-            for x in drained:
-                if passes[x][0]:
-                    square(x)
-            if k - LAG in pass_after:
-                latest = pass_after[k - LAG]
-                mx_passes(latest)
-                to_drain.append(latest)
-            for t in to_sum:
-                l2_matmuls(t, m_banks[latest][2])
-                to_copy.append((t, m_banks[latest][2]))
-            to_sum = []
-            for x in drained:
-                is_q, t, h0, n, members = passes[x]
-                if is_q and h0 + n == 4:
-                    to_sum.append(t)
+            if k < n_loads:
+                for t in complete:
+                    sum_squares(t)
+                    square_sums(t)
+            if next_run < len(runs) and runs[next_run][4] <= k:
+                mx_run(next_run)
+                to_drain.append(next_run)
+                next_run += 1
+            if k >= n_loads:
+                waiting.extend(complete)
+                if next_run == len(runs):
+                    for t in waiting:
+                        sum_squares(t)
+                        square_sums(t)
+                    waiting = []
 
+        nc.vector.tensor_tensor(out=l2_sb[:, 0:8], in0=acc[:, 0, :], in1=acc[:, 1, :], op=ALU.add)
         fin = mpool.tile([P, 512], F32, tag="m0")
         nc.tensor.transpose(fin[:, 0:P], l2_sb[:], ident[:])
         z = const.tile([P, 4, NS], F32)

@@ -90,7 +90,6 @@ def tile_proto_kernel(tc, feature_map, weight2, scale, out):
             in_=weight2.rearrange("s q m -> (s q) m").rearrange("(j p) m -> p j m", p=P),
         )
         sc_bf = const.tile([P, 1], BF16)
-        nc.scalar.dma_start(out=sc_bf[:], in_=scale.partition_broadcast(P))
         for k in range(X_BUFS):
             load_next()
 
@@ -130,7 +129,6 @@ def tile_proto_kernel(tc, feature_map, weight2, scale, out):
         nc.vector.memset(w2c[:, NQ * SLOT :].bitcast(I32), 0)
         nc.vector.memset(w2s[:, NQ * SLOT :].bitcast(I32), 0)
         nc.vector.memset(l2_sb[:], 0.0)
-        nc.vector.tensor_scalar(out=sc_f[:], in0=sc_bf[:], scalar1=LOGIT_FACTOR, scalar2=None, op0=ALU.mult)
 
         w32 = w_in[:].bitcast(F32)
         for b in range(3):
@@ -308,12 +306,14 @@ def tile_proto_kernel(tc, feature_map, weight2, scale, out):
                 is_q, t, h0, n4, members = passes[x]
                 if is_q and h0 + n4 == 4 and (j + 1 == len(runs) or runs[j + 1][0] != x):
                     complete.append(t)
-            if k < n_loads:
-                n = loads[k][1]
-                transposes(k)
-                for il in range(n):
+            turn = [k] if k < n_loads - 2 else ([k, k + 1] if k == n_loads - 2 else [])
+            for kk in turn:
+                transposes(kk)
+                for il in range(loads[kk][1]):
                     if len(x_tiles) < len(images):
                         load_next()
+                        if len(x_tiles) == len(images):
+                            nc.sync.dma_start(out=sc_bf[:], in_=scale.partition_broadcast(P))
             if not ending and 0 <= k - 1:
                 quantise(k - 1)
             if k in W2_SLOTS:
@@ -323,9 +323,9 @@ def tile_proto_kernel(tc, feature_map, weight2, scale, out):
                     scales=w2s[:, 1024 * half : 1024 * half + 1024],
                     in_=wg[2 + half][:],
                 )
-            if k < n_loads:
-                for b in range((DC * n + 1) // 2):
-                    copy_bank(k, b)
+            for kk in turn:
+                for b in range((DC * loads[kk][1] + 1) // 2):
+                    copy_bank(kk, b)
             if k < n_loads:
                 for t in complete:
                     sum_squares(t)
@@ -342,6 +342,7 @@ def tile_proto_kernel(tc, feature_map, weight2, scale, out):
                         square_sums(t)
                     waiting = []
 
+        nc.vector.tensor_scalar(out=sc_f[:], in0=sc_bf[:], scalar1=LOGIT_FACTOR, scalar2=None, op0=ALU.mult)
         nc.vector.tensor_tensor(out=l2_sb[:, 0:8], in0=acc[:, 0, :], in1=acc[:, 1, :], op=ALU.add)
         fin = mpool.tile([P, 512], F32, tag="m0")
         nc.tensor.transpose(fin[:, 0:P], l2_sb[:], ident[:])

@@ -28,8 +28,11 @@ LOGIT_FACTOR = -1.0 / (600.0 * 512.0 * 512.0)
 PIECES = {2: (8, 2), 1: (4, 1)}
 VECTOR_BANKS = {2: (4,), 1: (2,)}
 FULL_QUAD = ((2, 2),)
-QUERY_QUADS = (FULL_QUAD,) * 7 + (((2,), (1, 1)),)
-W2_SLOTS = (2, 3)
+SUPPORT_QUADS = (FULL_QUAD,) * 5 + (((2,), (1, 1)),)
+IDLE_FROM = 1
+IDLE_TO = 3
+IDLE_EACH = 3
+W1_SLOTS = (2, 3)
 
 
 def tile_proto_kernel(tc, feature_map, weight2, scale, out):
@@ -37,7 +40,7 @@ def tile_proto_kernel(tc, feature_map, weight2, scale, out):
     loads = []
     passes = []
     images = []
-    for is_q, quads in ((False, (FULL_QUAD,) * (NS // 4)), (True, QUERY_QUADS)):
+    for is_q, quads in ((True, (FULL_QUAD,) * (NQ // 4)), (False, SUPPORT_QUADS)):
         for t, quad in enumerate(quads):
             h0 = 0
             for group in quad:
@@ -93,12 +96,12 @@ def tile_proto_kernel(tc, feature_map, weight2, scale, out):
         for k in range(X_BUFS):
             load_next()
 
-        ident = const.tile([P, P], F32)
-        make_identity(nc, ident[:])
+        ident_t = const.tile([P, P], F32)
+        make_identity(nc, ident_t[:])
+        ident = ident_t[:]
         diffs = []
         for r in range(3):
             dt_r = const.tile([P, DC * P], F32, name="diff%d" % r)
-            nc.gpsimd.memset(dt_r[:], 0.0)
             diffs.append(dt_r)
 
         warm = const.tile([P, 1], F32)
@@ -109,11 +112,11 @@ def tile_proto_kernel(tc, feature_map, weight2, scale, out):
         w1s = const.tile([P, (NS + 1) * SLOT], U8, align_bytes=64)
         w2c = const.tile([P, (NQ + 1) * SLOT], U32, align_bytes=64)
         w2s = const.tile([P, (NQ + 1) * SLOT], U8, align_bytes=64)
-        c_sb = const.tile([P, DC * NQ * NS], F32)
-        l2_sb = const.tile([P, P], F32)
+        r_sb = const.tile([P, DC * NS * NQ], F32)
+        l2_sb = const.tile([P, 8], F32)
         acc = const.tile([P, 2, 8], F32)
         sc_f = const.tile([P, 1], F32)
-        cv = c_sb[:].rearrange("p (c q s) -> p c q s", c=DC, q=NQ, s=NS)
+        rv = r_sb[:].rearrange("p (c s q) -> p c s q", c=DC, s=NS, q=NQ)
 
         wg = []
         for r, slots in enumerate((16, 8, 16, 16)):
@@ -128,7 +131,12 @@ def tile_proto_kernel(tc, feature_map, weight2, scale, out):
         nc.vector.memset(wgv[3][:, :, NS:SLOT, :], 0.0)
         nc.vector.memset(w2c[:, NQ * SLOT :].bitcast(I32), 0)
         nc.vector.memset(w2s[:, NQ * SLOT :].bitcast(I32), 0)
-        nc.vector.memset(l2_sb[:], 0.0)
+
+        group = const.tile([P, 4], F32)
+        fold = const.tile([P, P], F32)
+        nc.vector.tensor_reduce(out=group[:], in_=ident.rearrange("p (i m) -> p i m", i=4, m=32), axis=AX.X, op=ALU.add)
+        nc.vector.memset(fold[:], 0.0)
+        nc.vector.tensor_reduce(out=fold[:, 0:32], in_=ident.rearrange("p (i m) -> p m i", i=4, m=32), axis=AX.X, op=ALU.add)
 
         w32 = w_in[:].bitcast(F32)
         for b in range(3):
@@ -138,7 +146,7 @@ def tile_proto_kernel(tc, feature_map, weight2, scale, out):
                     nc.tensor.transpose(
                         wb[:, (2 * cl + u) * P : (2 * cl + u + 1) * P],
                         w32[:, 2 * b + cl, u * P : (u + 1) * P],
-                        ident[:],
+                        ident,
                     )
             on_scalar = b != 1
             wb_sq = wb[:].rearrange("p (c u s q) -> p c s q u", c=2, u=2, s=4, q=NQ)
@@ -153,8 +161,21 @@ def tile_proto_kernel(tc, feature_map, weight2, scale, out):
                         wgv[2 + half][:, :, s0 : s0 + 4, :],
                         wb_qs[:, cl, 16 * half : 16 * half + 16],
                     )
-        nc.vector.quantize_mx(out=w1c[:, 0:1024].bitcast(FP8X4), scales=w1s[:, 0:1024], in_=wg[0][:])
-        nc.vector.quantize_mx(out=w1c[:, 1024:1536].bitcast(FP8X4), scales=w1s[:, 1024:1536], in_=wg[1][:])
+        nc.vector.quantize_mx(out=w2c[:, 0:1024].bitcast(FP8X4), scales=w2s[:, 0:1024], in_=wg[2][:])
+        nc.vector.quantize_mx(out=w2c[:, 1024:2048].bitcast(FP8X4), scales=w2s[:, 1024:2048], in_=wg[3][:])
+
+        def idle_passes(count):
+            sink = mpool.tile([P, 512], F32, tag="m1")
+            for r in range(count):
+                nc.tensor.matmul_mx(
+                    out=sink[:],
+                    lhsT=w2c[:, 0:P].bitcast(FP8X4),
+                    lhsT_scale=w2s[:, 0:P],
+                    rhs=w2c[:, 0:512].bitcast(FP8X4),
+                    rhs_scale=w2s[:, 0:512],
+                    start=True,
+                    stop=True,
+                )
 
         t_banks = {}
         grouped = {}
@@ -183,7 +204,7 @@ def tile_proto_kernel(tc, feature_map, weight2, scale, out):
                         nc.tensor.transpose(
                             tb[:, (2 * cl + h) * P : (2 * cl + h + 1) * P],
                             x32[:, dc * 256 + h * P : dc * 256 + (h + 1) * P],
-                            ident[:],
+                            ident,
                         )
                 banks.append(tb)
             t_banks[k] = banks
@@ -222,7 +243,7 @@ def tile_proto_kernel(tc, feature_map, weight2, scale, out):
                 dt_ps = tpool.tile([P, 512], F32, tag="tb")
                 for dc in range(c0, c1):
                     nc.tensor.transpose(
-                        dt_ps[:, (dc - c0) * P : (dc - c0 + 1) * P], diffs[t % 3][:, dc * P : (dc + 1) * P], ident[:]
+                        dt_ps[:, (dc - c0) * P : (dc - c0 + 1) * P], diffs[t % 3][:, dc * P : (dc + 1) * P], ident
                     )
                 turned[(t, part)] = dt_ps
 
@@ -267,8 +288,8 @@ def tile_proto_kernel(tc, feature_map, weight2, scale, out):
         def diff_view(j):
             x, d0, step, count, ready = runs[j]
             is_q, t, h0, n, members = passes[x]
-            dv = diffs[t % 3][:].rearrange("p (c i s) -> p c i s", c=DC, i=4, s=32)
-            return dv[:, d0 : d0 + step * (count - 1) + 1 : step, h0 : h0 + n, 0:NS]
+            dv = diffs[t % 3][:].rearrange("p (c i q) -> p c i q", c=DC, i=4, q=NQ)
+            return dv[:, d0 : d0 + step * (count - 1) + 1 : step, h0 : h0 + n, :]
 
         def drain(j):
             x, d0, step, count, ready = runs[j]
@@ -277,16 +298,16 @@ def tile_proto_kernel(tc, feature_map, weight2, scale, out):
             stop = d0 + step * (count - 1) + 1
             used = m_bank[j][:, 0 : count * n * BLK]
             if is_q:
-                nc.vector.tensor_tensor(
-                    out=diff_view(j),
-                    in0=cv[:, d0:stop:step, first : first + n, :],
-                    in1=used.rearrange("p (c i r) -> p c i r", c=count, i=n, r=BLK)[:, :, :, 0:NS],
-                    op=ALU.subtract,
+                nc.vector.tensor_copy(
+                    out=rv[:, d0:stop:step, :, first : first + n],
+                    in_=used.rearrange("p (c i r) -> p c r i", c=count, i=n, r=BLK)[:, :, 0:NS, :],
                 )
             else:
-                nc.vector.tensor_copy(
-                    out=cv[:, d0:stop:step, :, first : first + n],
-                    in_=used.rearrange("p (c i r) -> p c r i", c=count, i=n, r=BLK),
+                nc.vector.tensor_tensor(
+                    out=diff_view(j),
+                    in0=rv[:, d0:stop:step, first : first + n, :],
+                    in1=used.rearrange("p (c i r) -> p c i r", c=count, i=n, r=BLK),
+                    op=ALU.subtract,
                 )
 
         to_drain = []
@@ -304,7 +325,7 @@ def tile_proto_kernel(tc, feature_map, weight2, scale, out):
             for j in drained:
                 x = runs[j][0]
                 is_q, t, h0, n4, members = passes[x]
-                if is_q and h0 + n4 == 4 and (j + 1 == len(runs) or runs[j + 1][0] != x):
+                if not is_q and h0 + n4 == 4 and (j + 1 == len(runs) or runs[j + 1][0] != x):
                     complete.append(t)
             turn = [k] if k < n_loads - 2 else ([k, k + 1] if k == n_loads - 2 else [])
             for kk in turn:
@@ -316,12 +337,13 @@ def tile_proto_kernel(tc, feature_map, weight2, scale, out):
                             nc.sync.dma_start(out=sc_bf[:], in_=scale.partition_broadcast(P))
             if not ending and 0 <= k - 1:
                 quantise(k - 1)
-            if k in W2_SLOTS:
-                half = W2_SLOTS.index(k)
+            if k in W1_SLOTS:
+                half = W1_SLOTS.index(k)
+                cols = 1024 - 512 * half
                 nc.vector.quantize_mx(
-                    out=w2c[:, 1024 * half : 1024 * half + 1024].bitcast(FP8X4),
-                    scales=w2s[:, 1024 * half : 1024 * half + 1024],
-                    in_=wg[2 + half][:],
+                    out=w1c[:, 1024 * half : 1024 * half + cols].bitcast(FP8X4),
+                    scales=w1s[:, 1024 * half : 1024 * half + cols],
+                    in_=wg[half][:],
                 )
             for kk in turn:
                 for b in range((DC * loads[kk][1] + 1) // 2):
@@ -330,6 +352,8 @@ def tile_proto_kernel(tc, feature_map, weight2, scale, out):
                 for t in complete:
                     sum_squares(t)
                     square_sums(t)
+            if IDLE_FROM <= k < IDLE_TO:
+                idle_passes(IDLE_EACH)
             if next_run < len(runs) and runs[next_run][4] <= k:
                 mx_run(next_run)
                 to_drain.append(next_run)
@@ -343,30 +367,33 @@ def tile_proto_kernel(tc, feature_map, weight2, scale, out):
                     waiting = []
 
         nc.vector.tensor_scalar(out=sc_f[:], in0=sc_bf[:], scalar1=LOGIT_FACTOR, scalar2=None, op0=ALU.mult)
-        nc.vector.tensor_tensor(out=l2_sb[:, 0:8], in0=acc[:, 0, :], in1=acc[:, 1, :], op=ALU.add)
+        nc.vector.tensor_tensor(out=l2_sb[:, 0:6], in0=acc[:, 0, 0:6], in1=acc[:, 1, 0:6], op=ALU.add)
+        spread = const.tile([P, 4, 6], F32)
+        nc.vector.tensor_tensor(
+            out=spread[:],
+            in0=l2_sb[:, 0:6].unsqueeze(1).to_broadcast([P, 4, 6]),
+            in1=group[:].unsqueeze(2).to_broadcast([P, 4, 6]),
+            op=ALU.mult,
+        )
         fin = mpool.tile([P, 512], F32, tag="m0")
-        nc.tensor.transpose(fin[:, 0:P], l2_sb[:], ident[:])
-        z = const.tile([P, 4, NS], F32)
-        zs = const.tile([P, 4, NS], F32)
-        ez = const.tile([P, 4, NS], F32)
-        res = const.tile([P, 4, NS], F32)
-        mx = const.tile([P, 4], F32)
-        sm = const.tile([P, 4], F32)
-        ls = const.tile([P, 4], F32)
+        nc.tensor.matmul(out=fin[:, 0:NS], lhsT=fold[:], rhs=spread[:].rearrange("p i u -> p (i u)"), start=True, stop=True)
+        z = const.tile([P, NS], F32)
+        zs = const.tile([P, NS], F32)
+        ez = const.tile([P, NS], F32)
+        res = const.tile([P, NS], F32)
+        mx = const.tile([P, 1], F32)
+        sm = const.tile([P, 1], F32)
+        ls = const.tile([P, 1], F32)
         nc.vector.tensor_scalar(
-            out=z[:],
-            in0=fin[:, 0:P].rearrange("p (i s) -> p i s", i=4, s=32)[:, :, 0:NS],
+            out=z[:].rearrange("p (u i) -> p i u", u=6, i=4),
+            in0=fin[:, 0:NS].rearrange("p (i u) -> p i u", i=4, u=6),
             scalar1=sc_f[:, 0:1],
             scalar2=None,
             op0=ALU.mult,
         )
         nc.vector.tensor_reduce(out=mx[:], in_=z[:], axis=AX.X, op=ALU.max)
-        nc.vector.tensor_tensor(out=zs[:], in0=z[:], in1=mx[:].unsqueeze(2).to_broadcast([P, 4, NS]), op=ALU.subtract)
-        nc.scalar.activation(out=ez[:], in_=zs[:], func=ACT.Exp)
-        nc.vector.tensor_reduce(out=sm[:], in_=ez[:], axis=AX.X, op=ALU.add)
+        nc.vector.tensor_scalar(out=zs[:], in0=z[:], scalar1=mx[:, 0:1], scalar2=None, op0=ALU.subtract)
+        nc.scalar.activation(out=ez[:], in_=zs[:], func=ACT.Exp, accum_out=sm[:, 0:1])
         nc.scalar.activation(out=ls[:], in_=sm[:], func=ACT.Ln)
-        nc.vector.tensor_tensor(out=res[:], in0=zs[:], in1=ls[:].unsqueeze(2).to_broadcast([P, 4, NS]), op=ALU.subtract)
-        nc.sync.dma_start(
-            out=out.rearrange("(t l) s -> t (l s)", l=4),
-            in_=res[0:8].rearrange("p l s -> p (l s)"),
-        )
+        nc.vector.tensor_scalar(out=res[:], in0=zs[:], scalar1=ls[:, 0:1], scalar2=None, op0=ALU.subtract)
+        nc.sync.dma_start(out=out, in_=res[0:NQ, :])

@@ -29,9 +29,6 @@ PIECES = {2: (8, 2), 1: (4, 1)}
 VECTOR_BANKS = {2: (4,), 1: (2,)}
 FULL_QUAD = ((2, 2),)
 SUPPORT_QUADS = (FULL_QUAD,) * 5 + (((2,), (1, 1)),)
-IDLE_FROM = 1
-IDLE_TO = 3
-IDLE_EACH = 3
 W1_SLOTS = (2, 3)
 
 
@@ -163,19 +160,6 @@ def tile_proto_kernel(tc, feature_map, weight2, scale, out):
                     )
         nc.vector.quantize_mx(out=w2c[:, 0:1024].bitcast(FP8X4), scales=w2s[:, 0:1024], in_=wg[2][:])
         nc.vector.quantize_mx(out=w2c[:, 1024:2048].bitcast(FP8X4), scales=w2s[:, 1024:2048], in_=wg[3][:])
-
-        def idle_passes(count):
-            sink = mpool.tile([P, 512], F32, tag="m1")
-            for r in range(count):
-                nc.tensor.matmul_mx(
-                    out=sink[:],
-                    lhsT=w2c[:, 0:P].bitcast(FP8X4),
-                    lhsT_scale=w2s[:, 0:P],
-                    rhs=w2c[:, 0:512].bitcast(FP8X4),
-                    rhs_scale=w2s[:, 0:512],
-                    start=True,
-                    stop=True,
-                )
 
         t_banks = {}
         grouped = {}
@@ -352,8 +336,6 @@ def tile_proto_kernel(tc, feature_map, weight2, scale, out):
                 for t in complete:
                     sum_squares(t)
                     square_sums(t)
-            if IDLE_FROM <= k < IDLE_TO:
-                idle_passes(IDLE_EACH)
             if next_run < len(runs) and runs[next_run][4] <= k:
                 mx_run(next_run)
                 to_drain.append(next_run)

@@ -28,8 +28,8 @@ LOGIT_FACTOR = -1.0 / (600.0 * 512.0 * 512.0)
 PIECES = {2: (8, 2), 1: (4, 1)}
 VECTOR_BANKS = {2: (4,), 1: (2,)}
 FULL_QUAD = ((2, 2),)
-SUPPORT_QUADS = (FULL_QUAD,) * 5 + (((2,), (1, 1)),)
-W1_SLOTS = (2, 3)
+QUERY_QUADS = (FULL_QUAD,) * 7 + (((2,), (1, 1)),)
+W2_SLOTS = (2, 3)
 
 
 def tile_proto_kernel(tc, feature_map, weight2, scale, out):
@@ -37,7 +37,7 @@ def tile_proto_kernel(tc, feature_map, weight2, scale, out):
     loads = []
     passes = []
     images = []
-    for is_q, quads in ((True, (FULL_QUAD,) * (NQ // 4)), (False, SUPPORT_QUADS)):
+    for is_q, quads in ((False, (FULL_QUAD,) * (NS // 4)), (True, QUERY_QUADS)):
         for t, quad in enumerate(quads):
             h0 = 0
             for group in quad:
@@ -93,12 +93,12 @@ def tile_proto_kernel(tc, feature_map, weight2, scale, out):
         for k in range(X_BUFS):
             load_next()
 
-        ident_t = const.tile([P, P], F32)
-        make_identity(nc, ident_t[:])
-        ident = ident_t[:]
+        ident = const.tile([P, P], F32)
+        make_identity(nc, ident[:])
         diffs = []
         for r in range(3):
             dt_r = const.tile([P, DC * P], F32, name="diff%d" % r)
+            nc.gpsimd.memset(dt_r[:], 0.0)
             diffs.append(dt_r)
 
         warm = const.tile([P, 1], F32)
@@ -109,11 +109,11 @@ def tile_proto_kernel(tc, feature_map, weight2, scale, out):
         w1s = const.tile([P, (NS + 1) * SLOT], U8, align_bytes=64)
         w2c = const.tile([P, (NQ + 1) * SLOT], U32, align_bytes=64)
         w2s = const.tile([P, (NQ + 1) * SLOT], U8, align_bytes=64)
-        r_sb = const.tile([P, DC * NS * NQ], F32)
-        l2_sb = const.tile([P, 8], F32)
+        c_sb = const.tile([P, DC * NQ * NS], F32)
+        l2_sb = const.tile([P, P], F32)
         acc = const.tile([P, 2, 8], F32)
         sc_f = const.tile([P, 1], F32)
-        rv = r_sb[:].rearrange("p (c s q) -> p c s q", c=DC, s=NS, q=NQ)
+        cv = c_sb[:].rearrange("p (c s q) -> p c s q", c=DC, s=NS, q=NQ)
 
         wg = []
         for r, slots in enumerate((16, 8, 16, 16)):
@@ -128,12 +128,7 @@ def tile_proto_kernel(tc, feature_map, weight2, scale, out):
         nc.vector.memset(wgv[3][:, :, NS:SLOT, :], 0.0)
         nc.vector.memset(w2c[:, NQ * SLOT :].bitcast(I32), 0)
         nc.vector.memset(w2s[:, NQ * SLOT :].bitcast(I32), 0)
-
-        group = const.tile([P, 4], F32)
-        fold = const.tile([P, P], F32)
-        nc.vector.tensor_reduce(out=group[:], in_=ident.rearrange("p (i m) -> p i m", i=4, m=32), axis=AX.X, op=ALU.add)
-        nc.vector.memset(fold[:], 0.0)
-        nc.vector.tensor_reduce(out=fold[:, 0:32], in_=ident.rearrange("p (i m) -> p m i", i=4, m=32), axis=AX.X, op=ALU.add)
+        nc.vector.memset(l2_sb[:], 0.0)
 
         w32 = w_in[:].bitcast(F32)
         for b in range(3):
@@ -143,7 +138,7 @@ def tile_proto_kernel(tc, feature_map, weight2, scale, out):
                     nc.tensor.transpose(
                         wb[:, (2 * cl + u) * P : (2 * cl + u + 1) * P],
                         w32[:, 2 * b + cl, u * P : (u + 1) * P],
-                        ident,
+                        ident[:],
                     )
             on_scalar = b != 1
             wb_sq = wb[:].rearrange("p (c u s q) -> p c s q u", c=2, u=2, s=4, q=NQ)
@@ -158,8 +153,8 @@ def tile_proto_kernel(tc, feature_map, weight2, scale, out):
                         wgv[2 + half][:, :, s0 : s0 + 4, :],
                         wb_qs[:, cl, 16 * half : 16 * half + 16],
                     )
-        nc.vector.quantize_mx(out=w2c[:, 0:1024].bitcast(FP8X4), scales=w2s[:, 0:1024], in_=wg[2][:])
-        nc.vector.quantize_mx(out=w2c[:, 1024:2048].bitcast(FP8X4), scales=w2s[:, 1024:2048], in_=wg[3][:])
+        nc.vector.quantize_mx(out=w1c[:, 0:1024].bitcast(FP8X4), scales=w1s[:, 0:1024], in_=wg[0][:])
+        nc.vector.quantize_mx(out=w1c[:, 1024:1536].bitcast(FP8X4), scales=w1s[:, 1024:1536], in_=wg[1][:])
 
         t_banks = {}
         grouped = {}
@@ -188,7 +183,7 @@ def tile_proto_kernel(tc, feature_map, weight2, scale, out):
                         nc.tensor.transpose(
                             tb[:, (2 * cl + h) * P : (2 * cl + h + 1) * P],
                             x32[:, dc * 256 + h * P : dc * 256 + (h + 1) * P],
-                            ident,
+                            ident[:],
                         )
                 banks.append(tb)
             t_banks[k] = banks
@@ -227,7 +222,7 @@ def tile_proto_kernel(tc, feature_map, weight2, scale, out):
                 dt_ps = tpool.tile([P, 512], F32, tag="tb")
                 for dc in range(c0, c1):
                     nc.tensor.transpose(
-                        dt_ps[:, (dc - c0) * P : (dc - c0 + 1) * P], diffs[t % 3][:, dc * P : (dc + 1) * P], ident
+                        dt_ps[:, (dc - c0) * P : (dc - c0 + 1) * P], diffs[t % 3][:, dc * P : (dc + 1) * P], ident[:]
                     )
                 turned[(t, part)] = dt_ps
 
@@ -272,8 +267,8 @@ def tile_proto_kernel(tc, feature_map, weight2, scale, out):
         def diff_view(j):
             x, d0, step, count, ready = runs[j]
             is_q, t, h0, n, members = passes[x]
-            dv = diffs[t % 3][:].rearrange("p (c i q) -> p c i q", c=DC, i=4, q=NQ)
-            return dv[:, d0 : d0 + step * (count - 1) + 1 : step, h0 : h0 + n, :]
+            dv = diffs[t % 3][:].rearrange("p (c s i) -> p c s i", c=DC, s=32, i=4)
+            return dv[:, d0 : d0 + step * (count - 1) + 1 : step, 0:NS, h0 : h0 + n]
 
         def drain(j):
             x, d0, step, count, ready = runs[j]
@@ -282,16 +277,16 @@ def tile_proto_kernel(tc, feature_map, weight2, scale, out):
             stop = d0 + step * (count - 1) + 1
             used = m_bank[j][:, 0 : count * n * BLK]
             if is_q:
-                nc.vector.tensor_copy(
-                    out=rv[:, d0:stop:step, :, first : first + n],
-                    in_=used.rearrange("p (c i r) -> p c r i", c=count, i=n, r=BLK)[:, :, 0:NS, :],
-                )
-            else:
                 nc.vector.tensor_tensor(
                     out=diff_view(j),
-                    in0=rv[:, d0:stop:step, first : first + n, :],
-                    in1=used.rearrange("p (c i r) -> p c i r", c=count, i=n, r=BLK),
+                    in0=cv[:, d0:stop:step, :, first : first + n],
+                    in1=used.rearrange("p (c i r) -> p c r i", c=count, i=n, r=BLK)[:, :, 0:NS, :],
                     op=ALU.subtract,
+                )
+            else:
+                nc.vector.tensor_copy(
+                    out=cv[:, d0:stop:step, first : first + n, :],
+                    in_=used.rearrange("p (c i r) -> p c i r", c=count, i=n, r=BLK),
                 )
 
         to_drain = []
@@ -309,7 +304,7 @@ def tile_proto_kernel(tc, feature_map, weight2, scale, out):
             for j in drained:
                 x = runs[j][0]
                 is_q, t, h0, n4, members = passes[x]
-                if not is_q and h0 + n4 == 4 and (j + 1 == len(runs) or runs[j + 1][0] != x):
+                if is_q and h0 + n4 == 4 and (j + 1 == len(runs) or runs[j + 1][0] != x):
                     complete.append(t)
             turn = [k] if k < n_loads - 2 else ([k, k + 1] if k == n_loads - 2 else [])
             for kk in turn:
@@ -321,13 +316,12 @@ def tile_proto_kernel(tc, feature_map, weight2, scale, out):
                             nc.sync.dma_start(out=sc_bf[:], in_=scale.partition_broadcast(P))
             if not ending and 0 <= k - 1:
                 quantise(k - 1)
-            if k in W1_SLOTS:
-                half = W1_SLOTS.index(k)
-                cols = 1024 - 512 * half
+            if k in W2_SLOTS:
+                half = W2_SLOTS.index(k)
                 nc.vector.quantize_mx(
-                    out=w1c[:, 1024 * half : 1024 * half + cols].bitcast(FP8X4),
-                    scales=w1s[:, 1024 * half : 1024 * half + cols],
-                    in_=wg[half][:],
+                    out=w2c[:, 1024 * half : 1024 * half + 1024].bitcast(FP8X4),
+                    scales=w2s[:, 1024 * half : 1024 * half + 1024],
+                    in_=wg[2 + half][:],
                 )
             for kk in turn:
                 for b in range((DC * loads[kk][1] + 1) // 2):
@@ -349,33 +343,30 @@ def tile_proto_kernel(tc, feature_map, weight2, scale, out):
                     waiting = []
 
         nc.vector.tensor_scalar(out=sc_f[:], in0=sc_bf[:], scalar1=LOGIT_FACTOR, scalar2=None, op0=ALU.mult)
-        nc.vector.tensor_tensor(out=l2_sb[:, 0:6], in0=acc[:, 0, 0:6], in1=acc[:, 1, 0:6], op=ALU.add)
-        spread = const.tile([P, 4, 6], F32)
-        nc.vector.tensor_tensor(
-            out=spread[:],
-            in0=l2_sb[:, 0:6].unsqueeze(1).to_broadcast([P, 4, 6]),
-            in1=group[:].unsqueeze(2).to_broadcast([P, 4, 6]),
-            op=ALU.mult,
-        )
+        nc.vector.tensor_tensor(out=l2_sb[:, 0:8], in0=acc[:, 0, :], in1=acc[:, 1, :], op=ALU.add)
         fin = mpool.tile([P, 512], F32, tag="m0")
-        nc.tensor.matmul(out=fin[:, 0:NS], lhsT=fold[:], rhs=spread[:].rearrange("p i u -> p (i u)"), start=True, stop=True)
-        z = const.tile([P, NS], F32)
-        zs = const.tile([P, NS], F32)
-        ez = const.tile([P, NS], F32)
-        res = const.tile([P, NS], F32)
-        mx = const.tile([P, 1], F32)
-        sm = const.tile([P, 1], F32)
-        ls = const.tile([P, 1], F32)
+        nc.tensor.transpose(fin[:, 0:P], l2_sb[:], ident[:])
+        z = const.tile([P, 4, NS], F32)
+        zs = const.tile([P, 4, NS], F32)
+        ez = const.tile([P, 4, NS], F32)
+        res = const.tile([P, 4, NS], F32)
+        mx = const.tile([P, 4], F32)
+        sm = const.tile([P, 4], F32)
+        ls = const.tile([P, 4], F32)
         nc.vector.tensor_scalar(
-            out=z[:].rearrange("p (u i) -> p i u", u=6, i=4),
-            in0=fin[:, 0:NS].rearrange("p (i u) -> p i u", i=4, u=6),
+            out=z[:],
+            in0=fin[:, 0:P].rearrange("p (s i) -> p i s", s=32, i=4)[:, :, 0:NS],
             scalar1=sc_f[:, 0:1],
             scalar2=None,
             op0=ALU.mult,
         )
         nc.vector.tensor_reduce(out=mx[:], in_=z[:], axis=AX.X, op=ALU.max)
-        nc.vector.tensor_scalar(out=zs[:], in0=z[:], scalar1=mx[:, 0:1], scalar2=None, op0=ALU.subtract)
-        nc.scalar.activation(out=ez[:], in_=zs[:], func=ACT.Exp, accum_out=sm[:, 0:1])
+        nc.vector.tensor_tensor(out=zs[:], in0=z[:], in1=mx[:].unsqueeze(2).to_broadcast([P, 4, NS]), op=ALU.subtract)
+        nc.scalar.activation(out=ez[:], in_=zs[:], func=ACT.Exp)
+        nc.vector.tensor_reduce(out=sm[:], in_=ez[:], axis=AX.X, op=ALU.add)
         nc.scalar.activation(out=ls[:], in_=sm[:], func=ACT.Ln)
-        nc.vector.tensor_scalar(out=res[:], in0=zs[:], scalar1=ls[:, 0:1], scalar2=None, op0=ALU.subtract)
-        nc.sync.dma_start(out=out, in_=res[0:NQ, :])
+        nc.vector.tensor_tensor(out=res[:], in0=zs[:], in1=ls[:].unsqueeze(2).to_broadcast([P, 4, NS]), op=ALU.subtract)
+        nc.sync.dma_start(
+            out=out.rearrange("(t l) s -> t (l s)", l=4),
+            in_=res[0:8].rearrange("p l s -> p (l s)"),
+        )

@@ -68,7 +68,6 @@ def tile_proto_kernel(tc, feature_map, weight2, scale, out):
         tpool = ctx.enter_context(tc.psum_pool(name="tpool", bufs=6))
         mpool = ctx.enter_context(tc.psum_pool(name="mpool", bufs=1))
         jpool = ctx.enter_context(tc.tile_pool(name="jpool", bufs=2))
-        ctx.enter_context(tc.manual_schedule())
 
         x_tiles = []
 
@@ -113,7 +112,7 @@ def tile_proto_kernel(tc, feature_map, weight2, scale, out):
         l2_sb = const.tile([P, P], F32)
         acc = const.tile([P, 2, 8], F32)
         sc_f = const.tile([P, 1], F32)
-        cv = c_sb[:].rearrange("p (c s q) -> p c s q", c=DC, s=NS, q=NQ)
+        cv = c_sb[:].rearrange("p (c q s) -> p c q s", c=DC, q=NQ, s=NS)
 
         wg = []
         for r, slots in enumerate((16, 8, 16, 16)):
@@ -267,8 +266,8 @@ def tile_proto_kernel(tc, feature_map, weight2, scale, out):
         def diff_view(j):
             x, d0, step, count, ready = runs[j]
             is_q, t, h0, n, members = passes[x]
-            dv = diffs[t % 3][:].rearrange("p (c s i) -> p c s i", c=DC, s=32, i=4)
-            return dv[:, d0 : d0 + step * (count - 1) + 1 : step, 0:NS, h0 : h0 + n]
+            dv = diffs[t % 3][:].rearrange("p (c i s) -> p c i s", c=DC, i=4, s=32)
+            return dv[:, d0 : d0 + step * (count - 1) + 1 : step, h0 : h0 + n, 0:NS]
 
         def drain(j):
             x, d0, step, count, ready = runs[j]
@@ -279,14 +278,14 @@ def tile_proto_kernel(tc, feature_map, weight2, scale, out):
             if is_q:
                 nc.vector.tensor_tensor(
                     out=diff_view(j),
-                    in0=cv[:, d0:stop:step, :, first : first + n],
-                    in1=used.rearrange("p (c i r) -> p c r i", c=count, i=n, r=BLK)[:, :, 0:NS, :],
+                    in0=cv[:, d0:stop:step, first : first + n, :],
+                    in1=used.rearrange("p (c i r) -> p c i r", c=count, i=n, r=BLK)[:, :, :, 0:NS],
                     op=ALU.subtract,
                 )
             else:
                 nc.vector.tensor_copy(
-                    out=cv[:, d0:stop:step, first : first + n, :],
-                    in_=used.rearrange("p (c i r) -> p c i r", c=count, i=n, r=BLK),
+                    out=cv[:, d0:stop:step, :, first : first + n],
+                    in_=used.rearrange("p (c i r) -> p c r i", c=count, i=n, r=BLK),
                 )
 
         to_drain = []
@@ -355,7 +354,7 @@ def tile_proto_kernel(tc, feature_map, weight2, scale, out):
         ls = const.tile([P, 4], F32)
         nc.vector.tensor_scalar(
             out=z[:],
-            in0=fin[:, 0:P].rearrange("p (s i) -> p i s", s=32, i=4)[:, :, 0:NS],
+            in0=fin[:, 0:P].rearrange("p (i s) -> p i s", i=4, s=32)[:, :, 0:NS],
             scalar1=sc_f[:, 0:1],
             scalar2=None,
             op0=ALU.mult,

from contextlib import ExitStack

import concourse.mybir as mybir
from concourse.masks import make_identity

FLOPS = 2 * 2 * 24 * 32 * 640 * 512

F32 = mybir.dt.float32
BF16 = mybir.dt.bfloat16
U32 = mybir.dt.uint32
U8 = mybir.dt.uint8
I32 = mybir.dt.int32
FP8X4 = mybir.dt.float8_e4m3fn_x4
ALU = mybir.AluOpType
ACT = mybir.ActivationFunctionType
AX = mybir.AxisListType

P = 128
NS = 24
NQ = 32
DC = 5
X_BUFS = 14
SLOT = 64
LAG = 2
BLK = 32
LOGIT_FACTOR = -1.0 / (600.0 * 512.0 * 512.0)

PIECES = {2: (8, 2), 1: (4, 1)}
VECTOR_BANKS = {2: (4,), 1: (2,)}
FULL_QUAD = ((2, 2),)
QUERY_QUADS = (FULL_QUAD,) * 7 + (((2,), (1, 1)),)
W2_SLOTS = (2, 3)


def tile_proto_kernel(tc, feature_map, weight2, scale, out):
    nc = tc.nc
    loads = []
    passes = []
    images = []
    for is_q, quads in ((False, (FULL_QUAD,) * (NS // 4)), (True, QUERY_QUADS)):
        for t, quad in enumerate(quads):
            h0 = 0
            for group in quad:
                members = []
                for n in group:
                    members.append(len(loads))
                    loads.append((len(images), n))
                    for il in range(n):
                        images.append(4 * t + h0 + sum(loads[m][1] for m in members[:-1]) + il + (NS if is_q else 0))
                total = sum(group)
                passes.append((is_q, t, h0, total, members))
                h0 += total
    n_loads = len(loads)
    runs = []
    for x, entry in enumerate(passes):
        ready = entry[4][-1] + LAG
        if entry[3] == 4:
            runs.append((x, 0, 2, 3, ready))
            runs.append((x, 1, 2, 2, ready))
        else:
            runs.append((x, 0, 1, DC, ready))

    with ExitStack() as ctx:
        const = ctx.enter_context(tc.tile_pool(name="const", bufs=1))
        xin = ctx.enter_context(tc.tile_pool(name="xin", bufs=X_BUFS))
        gpool = ctx.enter_context(tc.tile_pool(name="gpool", bufs=4))
        qpool = ctx.enter_context(tc.tile_pool(name="qpool", bufs=5))
        tpool = ctx.enter_context(tc.psum_pool(name="tpool", bufs=6))
        mpool = ctx.enter_context(tc.psum_pool(name="mpool", bufs=1))
        jpool = ctx.enter_context(tc.tile_pool(name="jpool", bufs=2))

        x_tiles = []

        def load_next():
            img = images[len(x_tiles)]
            xt = xin.tile([P, DC * 512], BF16)
            nc.sync.dma_start(out=xt[:], in_=feature_map[img].rearrange("(p c) m -> p (c m)", c=DC))
            x_tiles.append(xt)

        def copy_words(on_scalar, dst, src):
            if on_scalar:
                nc.scalar.copy(out=dst, in_=src)
            else:
                nc.vector.tensor_copy(out=dst, in_=src)

        w_in = const.tile([P, 6, 512], BF16)
        nc.sync.dma_start(
            out=w_in[:],
            in_=weight2.rearrange("s q m -> (s q) m").rearrange("(j p) m -> p j m", p=P),
        )
        sc_bf = const.tile([P, 1], BF16)
        for k in range(X_BUFS):
            load_next()

        ident = const.tile([P, P], F32)
        make_identity(nc, ident[:])
        diffs = []
        for r in range(3):
            dt_r = const.tile([P, DC * P], F32, name="diff%d" % r)
            nc.gpsimd.memset(dt_r[:], 0.0)
            diffs.append(dt_r)

        warm = const.tile([P, 1], F32)
        nc.vector.memset(warm[:], 0.0)
        nc.scalar.activation(out=warm[:], in_=warm[:], func=ACT.Exp)

        w1c = const.tile([P, (NS + 1) * SLOT], U32, align_bytes=64)
        w1s = const.tile([P, (NS + 1) * SLOT], U8, align_bytes=64)
        w2c = const.tile([P, (NQ + 1) * SLOT], U32, align_bytes=64)
        w2s = const.tile([P, (NQ + 1) * SLOT], U8, align_bytes=64)
        c_sb = const.tile([P, DC * NQ * NS], F32)
        l2_sb = const.tile([P, P], F32)
        acc = const.tile([P, 2, 8], F32)
        sc_f = const.tile([P, 1], F32)
        cv = c_sb[:].rearrange("p (c q s) -> p c q s", c=DC, q=NQ, s=NS)

        wg = []
        for r, slots in enumerate((16, 8, 16, 16)):
            wg_r = const.tile([P, slots * SLOT * 4], BF16, align_bytes=64, name="wg%d" % r)
            wg.append(wg_r)
        wgv = [w[:].bitcast(F32).rearrange("p (l c u) -> p l c u", c=SLOT, u=2) for w in wg]
        nc.vector.memset(wgv[0][:, :, NQ:SLOT, :], 0.0)
        nc.vector.memset(wgv[1][:, :, NQ:SLOT, :], 0.0)
        nc.vector.memset(w1c[:, NS * SLOT :].bitcast(I32), 0)
        nc.vector.memset(w1s[:, NS * SLOT :].bitcast(I32), 0)
        nc.vector.memset(wgv[2][:, :, NS:SLOT, :], 0.0)
        nc.vector.memset(wgv[3][:, :, NS:SLOT, :], 0.0)
        nc.vector.memset(w2c[:, NQ * SLOT :].bitcast(I32), 0)
        nc.vector.memset(w2s[:, NQ * SLOT :].bitcast(I32), 0)
        nc.vector.memset(l2_sb[:], 0.0)

        w32 = w_in[:].bitcast(F32)
        for b in range(3):
            wb = tpool.tile([P, 512], F32, tag="tb")
            for cl in range(2):
                for u in range(2):
                    nc.tensor.transpose(
                        wb[:, (2 * cl + u) * P : (2 * cl + u + 1) * P],
                        w32[:, 2 * b + cl, u * P : (u + 1) * P],
                        ident[:],
                    )
            on_scalar = b != 1
            wb_sq = wb[:].rearrange("p (c u s q) -> p c s q u", c=2, u=2, s=4, q=NQ)
            wb_qs = wb[:].rearrange("p (c u s q) -> p c q s u", c=2, u=2, s=4, q=NQ)
            for cl in range(2):
                j = 2 * b + cl
                s0 = 4 * j
                copy_words(on_scalar, wgv[s0 // 16][:, s0 % 16 : s0 % 16 + 4, 0:NQ, :], wb_sq[:, cl])
                for half in range(2):
                    copy_words(
                        on_scalar,
                        wgv[2 + half][:, :, s0 : s0 + 4, :],
                        wb_qs[:, cl, 16 * half : 16 * half + 16],
                    )
        nc.vector.quantize_mx(out=w1c[:, 0:1024].bitcast(FP8X4), scales=w1s[:, 0:1024], in_=wg[0][:])
        nc.vector.quantize_mx(out=w1c[:, 1024:1536].bitcast(FP8X4), scales=w1s[:, 1024:1536], in_=wg[1][:])

        t_banks = {}
        grouped = {}
        quant = {}
        m_bank = {}
        turned = {}

        def piece_of(n, g):
            start = 0
            for pi, size in enumerate(PIECES[n]):
                if g < start + size:
                    return pi, g - start
                start += size
            return None

        def transposes(k):
            first, n = loads[k]
            banks = []
            for b in range((DC * n + 1) // 2):
                tb = tpool.tile([P, 512], F32, tag="tb")
                for cl in range(min(2, DC * n - 2 * b)):
                    g = 2 * b + cl
                    x32 = x_tiles[first + g // DC][:].bitcast(F32)
                    dc = g % DC
                    for h in range(2):
                        nc.tensor.transpose(
                            tb[:, (2 * cl + h) * P : (2 * cl + h + 1) * P],
                            x32[:, dc * 256 + h * P : dc * 256 + (h + 1) * P],
                            ident[:],
                        )
                banks.append(tb)
            t_banks[k] = banks
            g_big = gpool.tile([P, 4096], BF16, align_bytes=64)
            g_small = gpool.tile([P, 1024], BF16, align_bytes=64)
            grouped[k] = (g_big, g_small)

        def copy_bank(k, b):
            n = loads[k][1]
            chunks = min(2, DC * n - 2 * b)
            pi, c0 = piece_of(n, 2 * b)
            g32 = grouped[k][pi][:].bitcast(F32)
            copy_words(
                b not in VECTOR_BANKS[n],
                g32[:, c0 * 256 : (c0 + chunks) * 256].rearrange("p (c d h) -> p c d h", c=chunks, d=P, h=2),
                t_banks[k][b][:, 0 : chunks * 256].rearrange("p (c h d) -> p c d h", c=chunks, h=2, d=P),
            )

        def quantise(k):
            sizes = PIECES[loads[k][1]]
            c_big = qpool.tile([P, 1024], U32, align_bytes=64)
            p_big = qpool.tile([P, 1024], U8, align_bytes=64)
            c_small = qpool.tile([P, 256], U32, align_bytes=64)
            p_small = qpool.tile([P, 256], U8, align_bytes=64)
            quant[k] = ((c_big, p_big), (c_small, p_small))
            for pi, size in enumerate(sizes):
                codes, planes = quant[k][pi]
                nc.vector.quantize_mx(
                    out=codes[:, 0 : size * P].bitcast(FP8X4),
                    scales=planes[:, 0 : size * P],
                    in_=grouped[k][pi][:, 0 : size * 512],
                )

        def sum_squares(t):
            for part, (c0, c1) in enumerate(((0, 4), (4, DC))):
                dt_ps = tpool.tile([P, 512], F32, tag="tb")
                for dc in range(c0, c1):
                    nc.tensor.transpose(
                        dt_ps[:, (dc - c0) * P : (dc - c0 + 1) * P], diffs[t % 3][:, dc * P : (dc + 1) * P], ident[:]
                    )
                turned[(t, part)] = dt_ps

        def square_sums(t):
            for part, width in enumerate((4 * P, P)):
                junk = jpool.tile([P, 512], F32)
                nc.scalar.activation(
                    out=junk[:, 0:width],
                    in_=turned[(t, part)][:, 0:width],
                    func=ACT.Square,
                    accum_out=acc[:, part, t : t + 1],
                )

        def mx_run(j):
            x, d0, step, count, ready = runs[j]
            is_q, t, h0, n, members = passes[x]
            wc, ws = (w2c, w2s) if is_q else (w1c, w1s)
            where = []
            for k in members:
                for il in range(loads[k][1]):
                    where.append((k, il))
            mb = mpool.tile([P, 512], F32, tag="m%d" % (j % 2))
            for row in range(count):
                dc = d0 + step * row
                for i in range(n):
                    k, il = where[i]
                    pi, c0 = piece_of(loads[k][1], il * DC + dc)
                    codes, planes = quant[k][pi]
                    w0 = SLOT * (4 * t + h0 + i)
                    col = BLK * (row * n + i)
                    nc.tensor.matmul_mx(
                        out=mb[:, col : col + P],
                        lhsT=codes[:, c0 * P : (c0 + 1) * P].bitcast(FP8X4),
                        lhsT_scale=planes[:, c0 * P : (c0 + 1) * P],
                        rhs=wc[:, w0 : w0 + P].bitcast(FP8X4),
                        rhs_scale=ws[:, w0 : w0 + P],
                        start=True,
                        stop=True,
                    )
            m_bank[j] = mb

        def diff_view(j):
            x, d0, step, count, ready = runs[j]
            is_q, t, h0, n, members = passes[x]
            dv = diffs[t % 3][:].rearrange("p (c i s) -> p c i s", c=DC, i=4, s=32)
            return dv[:, d0 : d0 + step * (count - 1) + 1 : step, h0 : h0 + n, 0:NS]

        def drain(j):
            x, d0, step, count, ready = runs[j]
            is_q, t, h0, n, members = passes[x]
            first = 4 * t + h0
            stop = d0 + step * (count - 1) + 1
            used = m_bank[j][:, 0 : count * n * BLK]
            if is_q:
                nc.vector.tensor_tensor(
                    out=diff_view(j),
                    in0=cv[:, d0:stop:step, first : first + n, :],
                    in1=used.rearrange("p (c i r) -> p c i r", c=count, i=n, r=BLK)[:, :, :, 0:NS],
                    op=ALU.subtract,
                )
            else:
                nc.vector.tensor_copy(
                    out=cv[:, d0:stop:step, :, first : first + n],
                    in_=used.rearrange("p (c i r) -> p c r i", c=count, i=n, r=BLK),
                )

        to_drain = []
        next_run = 0
        waiting = []
        for k in range(n_loads + 8):
            ending = k >= n_loads - 1
            if ending and 0 <= k - 1 < n_loads:
                quantise(k - 1)
            drained = to_drain
            to_drain = []
            for j in drained:
                drain(j)
            complete = []
            for j in drained:
                x = runs[j][0]
                is_q, t, h0, n4, members = passes[x]
                if is_q and h0 + n4 == 4 and (j + 1 == len(runs) or runs[j + 1][0] != x):
                    complete.append(t)
            turn = [k] if k < n_loads - 2 else ([k, k + 1] if k == n_loads - 2 else [])
            for kk in turn:
                transposes(kk)
                for il in range(loads[kk][1]):
                    if len(x_tiles) < len(images):
                        load_next()
                        if len(x_tiles) == len(images):
                            nc.sync.dma_start(out=sc_bf[:], in_=scale.partition_broadcast(P))
            if not ending and 0 <= k - 1:
                quantise(k - 1)
            if k in W2_SLOTS:
                half = W2_SLOTS.index(k)
                nc.vector.quantize_mx(
                    out=w2c[:, 1024 * half : 1024 * half + 1024].bitcast(FP8X4),
                    scales=w2s[:, 1024 * half : 1024 * half + 1024],
                    in_=wg[2 + half][:],
                )
            for kk in turn:
                for b in range((DC * loads[kk][1] + 1) // 2):
                    copy_bank(kk, b)
            if k < n_loads:
                for t in complete:
                    sum_squares(t)
                    square_sums(t)
            if next_run < len(runs) and runs[next_run][4] <= k:
                mx_run(next_run)
                to_drain.append(next_run)
                next_run += 1
            if k >= n_loads:
                waiting.extend(complete)
                if next_run == len(runs):
                    for t in waiting:
                        sum_squares(t)
                        square_sums(t)
                    waiting = []

        nc.vector.tensor_scalar(out=sc_f[:], in0=sc_bf[:], scalar1=LOGIT_FACTOR, scalar2=None, op0=ALU.mult)
        nc.vector.tensor_tensor(out=l2_sb[:, 0:8], in0=acc[:, 0, :], in1=acc[:, 1, :], op=ALU.add)
        fin = mpool.tile([P, 512], F32, tag="m0")
        nc.tensor.transpose(fin[:, 0:P], l2_sb[:], ident[:])
        z = const.tile([P, 4, NS], F32)
        zs = const.tile([P, 4, NS], F32)
        ez = const.tile([P, 4, NS], F32)
        res = const.tile([P, 4, NS], F32)
        mx = const.tile([P, 4], F32)
        sm = const.tile([P, 4], F32)
        ls = const.tile([P, 4], F32)
        nc.vector.tensor_scalar(
            out=z[:],
            in0=fin[:, 0:P].rearrange("p (i s) -> p i s", i=4, s=32)[:, :, 0:NS],
            scalar1=sc_f[:, 0:1],
            scalar2=None,
            op0=ALU.mult,
        )
        nc.vector.tensor_reduce(out=mx[:], in_=z[:], axis=AX.X, op=ALU.max)
        nc.vector.tensor_tensor(out=zs[:], in0=z[:], in1=mx[:].unsqueeze(2).to_broadcast([P, 4, NS]), op=ALU.subtract)
        nc.scalar.activation(out=ez[:], in_=zs[:], func=ACT.Exp)
        nc.vector.tensor_reduce(out=sm[:], in_=ez[:], axis=AX.X, op=ALU.add)
        nc.scalar.activation(out=ls[:], in_=sm[:], func=ACT.Ln)
        nc.vector.tensor_tensor(out=res[:], in0=zs[:], in1=ls[:].unsqueeze(2).to_broadcast([P, 4, NS]), op=ALU.subtract)
        nc.sync.dma_start(
            out=out.rearrange("(t l) s -> t (l s)", l=4),
            in_=res[0:8].rearrange("p l s -> p (l s)"),
        )
